import numpy as np
import ml_dtypes


def mxq(x, axis, fmt="e4m3"):
    dtype, down = {"e4m3": (ml_dtypes.float8_e4m3fn, 7), "e5m2": (ml_dtypes.float8_e5m2, 14)}[fmt]
    v = np.moveaxis(np.asarray(x, np.float32).astype(ml_dtypes.bfloat16).astype(np.float64), axis, -1)
    blocks = v.reshape(v.shape[:-1] + (-1, 32))
    amax = np.abs(blocks).max(-1, keepdims=True)
    byte = np.maximum(np.where(amax > 0, np.frexp(amax)[1] - 1 + 127, 0) - down, 1)
    scale = np.exp2(byte - 127.0)
    codes = (blocks / scale).astype(np.float32).astype(dtype).astype(np.float64)
    return np.moveaxis((codes * scale).reshape(v.shape), -1, axis)


WIDE = False


def mx_kscale(k):
    if not WIDE:
        return np.ones(k)
    levels = np.array([10, -10, 5, -5, 0])
    a = np.random.permutation(np.resize(levels, k // 512 * 4)).reshape(k // 512, 4)
    idx = np.arange(k)
    return np.exp2(a[idx // 512, idx % 128 // 32])


BF16 = ml_dtypes.bfloat16


def bf(x):
    return np.asarray(x, np.float32).astype(BF16)


def f64(x):
    return np.asarray(x).astype(np.float64)


E2M1 = np.array([0.0, 0.5, 1.0, 1.5, 2.0, 3.0, 4.0, 6.0, -0.0, -0.5, -1.0, -1.5, -2.0, -3.0, -4.0, -6.0])


def pack_weight(w, fmt):
    k, n = w.shape
    w = f64(bf(w)).reshape(k // 32, 32, n)
    amax = np.abs(w).max(1)
    if fmt == "e4m3":
        byte = np.frexp(amax)[1] - 1 + 127 - 7
    else:
        mant, ex = np.frexp(amax / 6.0)
        byte = np.where(mant > 0.5, ex, ex - 1) + 127
    byte = np.clip(np.where(amax > 0, byte, 1), 1, 254)
    scaled = (w * np.exp2(127.0 - byte)[:, None, :]).reshape(k, n).astype(np.float32)
    by_word = np.ascontiguousarray(scaled.reshape(k // 512, 128, 4, n).transpose(0, 1, 3, 2))
    if fmt == "e4m3":
        words = by_word.astype(ml_dtypes.float8_e4m3fn).view(np.uint8)
    else:
        c = by_word.astype(ml_dtypes.float4_e2m1fn).view(np.uint8) & 0xF
        words = c[..., 0::2] | (c[..., 1::2] << 4)
    return np.ascontiguousarray(words), np.ascontiguousarray(byte.astype(np.uint8).reshape(k // 512, 16, n))


def unpack_weight(words, scales, fmt):
    g, p, n, _ = words.shape
    if fmt == "e4m3":
        vals = np.ascontiguousarray(words).view(ml_dtypes.float8_e4m3fn).astype(np.float64)
    else:
        nib = np.empty((g, p, n, 4), np.uint8)
        nib[..., 0::2] = words & 0xF
        nib[..., 1::2] = words >> 4
        vals = E2M1[nib]
    vals = vals * np.repeat(np.exp2(scales.astype(np.float64) - 127.0), 8, axis=1)[..., None]
    return vals.transpose(0, 1, 3, 2).reshape(g * 512, n)

def pack4(w):
    words, scales = pack_weight(w, "e2m1")
    return words.reshape(words.shape[0], 128, -1), scales


def unpack4(words, scales):
    return unpack_weight(words.reshape(words.shape[0], 128, -1, 2), scales, "e2m1")


B, C, CK, CV, CO, H, W, P1, P2, P3, P4 = 1, 1024, 256, 256, 1024, 24, 48, 1, 3, 6, 8
PSP_SIZES = (P1, P2, P3, P4)
EPS = 1e-5
N = H * W


def bnrelu(x, gamma, beta, mean, var):
    inv = 1.0 / np.sqrt(var + EPS)
    return np.maximum((x - mean[None, :, None]) * (inv * gamma)[None, :, None] + beta[None, :, None], 0.0)


def psp(x):
    b, c = x.shape[:2]
    outs = []
    for s in PSP_SIZES:
        outs.append(x.reshape(b, c, s, H // s, s, W // s).mean(axis=(3, 5)).reshape(b, c, s * s))
    return np.concatenate(outs, axis=-1)


def setup_inputs():
    s = mx_kscale(C)
    fine = np.random.standard_normal((B, C, H, W))
    coarse = np.random.standard_normal((B, C, P4, P4))
    coarse = np.repeat(np.repeat(coarse, H // P4, axis=2), W // P4, axis=3)
    feats = bf((fine + coarse) * np.sqrt(0.5) * s[None, :, None, None])
    wk = np.random.standard_normal((CK, C)) * 1.5 / np.sqrt(C) / s[None, :]
    bk = bf(np.random.standard_normal(CK) * 0.2)
    gk = bf(1.0 + 0.1 * np.random.standard_normal(CK))
    betak = bf(np.random.standard_normal(CK) * 0.2)
    mk = bf(np.random.standard_normal(CK) * 0.2)
    vk = bf(np.random.uniform(0.5, 1.5, CK))
    wv = np.random.standard_normal((CV, C)) / np.sqrt(C) / s[None, :]
    bv = bf(np.random.standard_normal(CV) * 0.2)
    wk_words, wk_scales = pack4(np.ascontiguousarray(wk.T))
    wv_words, wv_scales = pack4(np.ascontiguousarray(wv.T))
    return {"feats": feats,
            "Wk_words": wk_words,
            "Wk_scales": wk_scales,
            "bk": bk,
            "gk": gk,
            "betak": betak,
            "mk": mk,
            "vk": vk,
            "Wv_words": wv_words,
            "Wv_scales": wv_scales,
            "bv": bv}


def reference(feats, Wk_words, Wk_scales, bk, gk, betak, mk, vk, Wv_words, Wv_scales, bv):
    xq = mxq(f64(feats).reshape(B, C, N), 1, "e4m3")
    pre = (unpack4(Wk_words, Wk_scales).T @ xq) + f64(bk)[None, :, None]
    kf = bnrelu(pre, f64(gk), f64(betak), f64(mk), f64(vk)).reshape(B, CK, H, W)
    keyp = psp(kf)
    val = ((unpack4(Wv_words, Wv_scales).T @ xq) + f64(bv)[None, :, None]).reshape(B, CV, H, W)
    value = psp(val).transpose(0, 2, 1)
    return kf, keyp, value

@@ -1,0 +1,197 @@
+from contextlib import ExitStack
+
+import concourse.mybir as mybir
+from concourse.masks import make_identity
+
+BF16 = mybir.dt.bfloat16
+F32 = mybir.dt.float32
+I32 = mybir.dt.int32
+U8 = mybir.dt.uint8
+U32 = mybir.dt.uint32
+FP8X4 = mybir.dt.float8_e4m3fn_x4
+FP4X4 = mybir.dt.float4_e2m1fn_x4
+ADD = mybir.AluOpType.add
+MULT = mybir.AluOpType.mult
+ACT = mybir.ActivationFunctionType
+AXIS = mybir.AxisListType
+
+P = 128
+PACK = 4
+GROUPS = 2
+HEIGHT = 24
+WIDTH = 48
+POSITIONS = HEIGHT * WIDTH
+BAND_ROWS = 8
+BANDS = HEIGHT // BAND_ROWS
+BAND = BAND_ROWS * WIDTH
+SLICE = 128
+MAPS = 4
+LEVELS = (1, 3, 6, 8)
+TOKENS = 110
+EPS = 1e-5
+VECTOR_BLOCKS = 32
+
+FLOPS = 2 * 512 * 1024 * POSITIONS
+
+
+def tile_apnb_pa_kernel(
+    tc, feats, Wk_words, Wk_scales, bk, gk, betak, mk, vk, Wv_words, Wv_scales, bv, out_0, out_1, out_2
+):
+    nc = tc.nc
+    first_token = {1: 0, 3: 1, 6: 10, 8: 46}
+    with ExitStack() as ctx:
+        keep = ctx.enter_context(tc.tile_pool(name="keep", bufs=1))
+        psum = ctx.enter_context(tc.psum_pool(name="psum", bufs=1))
+
+        x_rows = feats[0].rearrange("(g p t) h w -> g p t (h w)", p=P, t=PACK)
+        raw = {}
+
+        def load_band(band):
+            for g in range(GROUPS):
+                raw[g, band] = keep.tile([P, PACK, BAND], BF16, name="raw_%d_%d" % (g, band))
+                nc.sync.dma_start(out=raw[g, band][:], in_=x_rows[g, :, :, band * BAND : (band + 1) * BAND])
+
+        w_words = keep.tile([P, 2, GROUPS, 4 * P], U8, align_bytes=64)
+        w_planes = keep.tile([P, 2, GROUPS, 2 * P], U8, align_bytes=64)
+        nc.vector.memset(w_planes[:].bitcast(I32), 0)
+        vec_rows = keep.tile([P, P], BF16)
+        nc.vector.memset(vec_rows[:], 0.0)
+
+        load_band(0)
+        for wt, (words, scales_in) in enumerate(((Wk_words, Wk_scales), (Wv_words, Wv_scales))):
+            for quad in range(4):
+                nc.sync.dma_start(
+                    out=w_planes[32 * quad : 32 * quad + 4, wt].bitcast(I32),
+                    in_=scales_in.bitcast(I32)[:, 4 * quad : 4 * quad + 4, :].rearrange("g r n -> r g n"),
+                )
+            nc.sync.dma_start(out=w_words[:, wt].bitcast(I32), in_=words.bitcast(I32).rearrange("g p n -> p g n"))
+        load_band(1)
+        load_band(2)
+        for v, vec in enumerate((bk, gk, betak, mk, vk, bv)):
+            nc.scalar.dma_start(out=vec_rows[2 * v : 2 * v + 2, :], in_=vec.rearrange("(m c) -> m c", m=2))
+
+        ident = keep.tile([P, P], F32)
+        make_identity(nc, ident[:])
+        ident_bf = keep.tile([P, P], BF16)
+        nc.vector.tensor_copy(out=ident_bf[:], in_=ident[:])
+        ones = keep.tile([P, P], F32)
+        nc.vector.memset(ones[:], 1.0)
+        inv_size = keep.tile([P, P], F32)
+        nc.vector.memset(inv_size[:], 0.0)
+        for s in LEVELS:
+            cells = slice(first_token[s], first_token[s] + s * s)
+            nc.vector.tensor_scalar_mul(out=inv_size[:, cells], in0=ones[:, cells], scalar1=float(s * s) / POSITIONS)
+        tok = keep.tile([P, MAPS, P], F32)
+        nc.vector.memset(tok[:], 0.0)
+
+        vec_t = psum.tile([P, P], BF16, tag="vec_t")
+        nc.tensor.transpose(vec_t[:], vec_rows[:], ident_bf[:])
+        per_ch = keep.tile([P, 12], F32)
+        nc.vector.tensor_copy(out=per_ch[:], in_=vec_t[:, 0:12])
+        bk_c, gk_c, betak_c, mk_c, vk_c, bv_c = [per_ch[:, 2 * v : 2 * v + 2] for v in range(6)]
+        var_eps = keep.tile([P, 2], F32)
+        nc.vector.tensor_scalar_add(out=var_eps[:], in0=vk_c, scalar1=EPS)
+        std = keep.tile([P, 2], F32)
+        nc.scalar.activation(out=std[:], in_=var_eps[:], func=ACT.Sqrt)
+        inv_std = keep.tile([P, 2], F32)
+        nc.vector.reciprocal(out=inv_std[:], in_=std[:])
+        gain = keep.tile([P, 2], F32)
+        nc.vector.tensor_mul(out=gain[:], in0=inv_std[:], in1=gk_c)
+        centred = keep.tile([P, 2], F32)
+        nc.vector.tensor_sub(out=centred[:], in0=bk_c, in1=mk_c)
+        scaled = keep.tile([P, 2], F32)
+        nc.vector.tensor_mul(out=scaled[:], in0=centred[:], in1=gain[:])
+        shift = keep.tile([P, 2], F32)
+        nc.vector.tensor_add(out=shift[:], in0=scaled[:], in1=betak_c)
+
+        kf_out = out_0[0].rearrange("(m p) h w -> p m (h w)", p=P)
+        row_sums8 = keep.tile([P, MAPS, HEIGHT * 8], F32)
+
+        for band in range(BANDS):
+            grouped = keep.tile([P, GROUPS, BAND, PACK], BF16, name="grouped_%d" % band, align_bytes=64)
+            for g in range(GROUPS):
+                src = raw[g, band][:].rearrange("p t (c i) -> p c t i", i=4)
+                dst = grouped[:, g].rearrange("p (c i) t -> p c t i", i=4)
+                nc.vector.tensor_copy(out=dst[:, 0:VECTOR_BLOCKS], in_=src[:, 0:VECTOR_BLOCKS])
+                nc.scalar.copy(out=dst[:, VECTOR_BLOCKS:], in_=src[:, VECTOR_BLOCKS:])
+            codes = keep.tile([P, GROUPS * BAND], U32, name="codes_%d" % band, align_bytes=64)
+            scales = keep.tile([P, GROUPS * BAND], U8, name="scales_%d" % band, align_bytes=64)
+            flat = grouped[:].rearrange("p g c t -> p (g c t)")
+            for first, width in ((0, 512), (512, 256)):
+                nc.vector.quantize_mx(
+                    out=codes[:, first : first + width].bitcast(FP8X4),
+                    scales=scales[:, first : first + width],
+                    in_=flat[:, PACK * first : PACK * (first + width)],
+                )
+
+            maps = keep.tile([P, MAPS, BAND], F32, name="maps_%d" % band)
+            for q in range(MAPS):
+                wt, m = divmod(q, 2)
+                acc = psum.tile([P, BAND], F32, tag="acc", bufs=6)
+                for s in range(BAND // SLICE):
+                    for g in range(GROUPS):
+                        cols = slice(g * BAND + s * SLICE, g * BAND + (s + 1) * SLICE)
+                        nc.tensor.matmul_mx(
+                            out=acc[:, s * SLICE : (s + 1) * SLICE],
+                            lhsT=w_words[:, wt, g, 2 * P * m : 2 * P * (m + 1)].bitcast(FP4X4),
+                            lhsT_scale=w_planes[:, wt, g, P * m : P * (m + 1)],
+                            rhs=codes[:, cols].bitcast(FP8X4),
+                            rhs_scale=scales[:, cols],
+                            start=(g == 0),
+                            stop=(g == GROUPS - 1),
+                        )
+                if wt == 0:
+                    nc.scalar.activation(
+                        out=maps[:, q, :], in_=acc[:], func=ACT.Relu, bias=shift[:, m : m + 1], scale=gain[:, m : m + 1]
+                    )
+                else:
+                    nc.scalar.activation(out=maps[:, q, :], in_=acc[:], func=ACT.Identity, bias=bv_c[:, m : m + 1])
+            nc.sync.dma_start(out=kf_out[:, :, band * BAND : (band + 1) * BAND], in_=maps[:, 0:2, :])
+
+            halves = maps[:].rearrange("p q (n two) -> p q n two", two=2)
+            pair = keep.tile([P, MAPS, BAND // 2], F32, name="pair_%d" % band)
+            nc.vector.tensor_tensor(out=pair[:], in0=halves[:, :, :, 0], in1=halves[:, :, :, 1], op=ADD)
+            for a in (2 * band, 2 * band + 1):
+                rows = pair[:, :, 96 * (a - 2 * band) : 96 * (a - 2 * band + 1)]
+                nc.vector.tensor_reduce(
+                    out=tok[:, :, first_token[6] + 6 * a : first_token[6] + 6 * (a + 1)],
+                    in_=rows.rearrange("p q (i b j) -> p q b i j", i=4, b=6, j=4),
+                    axis=AXIS.XY,
+                    op=ADD,
+                )
+            nc.vector.tensor_reduce(
+                out=row_sums8[:, :, 64 * band : 64 * (band + 1)],
+                in_=pair[:].rearrange("p q (n j) -> p q n j", j=3),
+                axis=AXIS.X,
+                op=ADD,
+            )
+            a_done, a_new = (BAND_ROWS * band) // 3, (BAND_ROWS * (band + 1)) // 3
+            nc.vector.tensor_reduce(
+                out=tok[:, :, first_token[8] + 8 * a_done : first_token[8] + 8 * a_new].rearrange(
+                    "p q (a b) -> p q a b", b=8
+                ),
+                in_=row_sums8[:, :, 24 * a_done : 24 * a_new].rearrange("p q (a i b) -> p q a b i", i=3, b=8),
+                axis=AXIS.X,
+                op=ADD,
+            )
+            nc.vector.tensor_reduce(
+                out=tok[:, :, first_token[3] + 3 * band : first_token[3] + 3 * (band + 1)],
+                in_=tok[:, :, first_token[6] + 12 * band : first_token[6] + 12 * (band + 1)].rearrange(
+                    "p q (a b j) -> p q b a j", a=2, b=3, j=2
+                ),
+                axis=AXIS.XY,
+                op=ADD,
+            )
+        nc.vector.tensor_reduce(out=tok[:, :, 0], in_=tok[:, :, 1:10], axis=AXIS.X, op=ADD)
+
+        means = keep.tile([P, MAPS, P], F32)
+        both = inv_size[:].unsqueeze(1).to_broadcast([P, 2, P])
+        nc.vector.tensor_tensor(out=means[:, 2:4, :], in0=tok[:, 2:4, :], in1=both, op=MULT)
+        nc.vector.tensor_tensor(out=means[:, 0:2, :], in0=tok[:, 0:2, :], in1=both, op=MULT)
+        value_t = psum.tile([P, 2 * P], F32, tag="value_t")
+        for m in range(2):
+            nc.tensor.transpose(value_t[:, m * P : (m + 1) * P], means[:, 2 + m, :], ident[:])
+        value_sb = keep.tile([P, 2 * P], F32)
+        nc.scalar.copy(out=value_sb[:], in_=value_t[:])
+        nc.sync.dma_start(out=out_2[0], in_=value_sb[0:TOKENS, :])
+        nc.sync.dma_start(out=out_1[0].rearrange("(m p) t -> p m t", p=P), in_=means[:, 0:2, 0:TOKENS])

@@ -12,6 +12,7 @@ FP8X4 = mybir.dt.float8_e4m3fn_x4
 FP4X4 = mybir.dt.float4_e2m1fn_x4
 ADD = mybir.AluOpType.add
 MULT = mybir.AluOpType.mult
+NOT_EQUAL = mybir.AluOpType.not_equal
 ACT = mybir.ActivationFunctionType
 AXIS = mybir.AxisListType
 
@@ -25,11 +26,13 @@ BAND_ROWS = 8
 BANDS = HEIGHT // BAND_ROWS
 BAND = BAND_ROWS * WIDTH
 SLICE = 128
-MAPS = 4
+SLICES = BAND // SLICE
+BLOCKS = POSITIONS // SLICE
+HALVES = 2
 LEVELS = (1, 3, 6, 8)
 TOKENS = 110
 EPS = 1e-5
-VECTOR_BLOCKS = 32
+AHEAD = 2
 
 FLOPS = 2 * 512 * 1024 * POSITIONS
 
@@ -42,115 +45,94 @@ def tile_apnb_pa_kernel(
     with ExitStack() as ctx:
         keep = ctx.enter_context(tc.tile_pool(name="keep", bufs=1))
         psum = ctx.enter_context(tc.psum_pool(name="psum", bufs=1))
+        ctx.enter_context(tc.manual_schedule())
 
         x_rows = feats[0].rearrange("(g p t) h w -> g p t (h w)", p=P, t=PACK)
+        kf_out = out_0[0].rearrange("(m p) h w -> p m (h w)", p=P)
         raw = {}
+        codes = {}
+        scales = {}
+        kf = {}
+        val = {}
 
         def load_band(band):
             for g in range(GROUPS):
                 raw[g, band] = keep.tile([P, PACK, BAND], BF16, name="raw_%d_%d" % (g, band))
                 nc.sync.dma_start(out=raw[g, band][:], in_=x_rows[g, :, :, band * BAND : (band + 1) * BAND])
 
-        w_words = keep.tile([P, 2, GROUPS, 4 * P], U8, align_bytes=64)
-        w_planes = keep.tile([P, 2, GROUPS, 2 * P], U8, align_bytes=64)
-        nc.vector.memset(w_planes[:].bitcast(I32), 0)
-        vec_rows = keep.tile([P, P], BF16)
-        nc.vector.memset(vec_rows[:], 0.0)
-
-        load_band(0)
-        for wt, (words, scales_in) in enumerate(((Wk_words, Wk_scales), (Wv_words, Wv_scales))):
-            for quad in range(4):
-                nc.sync.dma_start(
-                    out=w_planes[32 * quad : 32 * quad + 4, wt].bitcast(I32),
-                    in_=scales_in.bitcast(I32)[:, 4 * quad : 4 * quad + 4, :].rearrange("g r n -> r g n"),
-                )
-            nc.sync.dma_start(out=w_words[:, wt].bitcast(I32), in_=words.bitcast(I32).rearrange("g p n -> p g n"))
-        load_band(1)
-        load_band(2)
-        for v, vec in enumerate((bk, gk, betak, mk, vk, bv)):
-            nc.scalar.dma_start(out=vec_rows[2 * v : 2 * v + 2, :], in_=vec.rearrange("(m c) -> m c", m=2))
-
-        ident = keep.tile([P, P], F32)
-        make_identity(nc, ident[:])
-        ident_bf = keep.tile([P, P], BF16)
-        nc.vector.tensor_copy(out=ident_bf[:], in_=ident[:])
-        ones = keep.tile([P, P], F32)
-        nc.vector.memset(ones[:], 1.0)
-        inv_size = keep.tile([P, P], F32)
-        nc.vector.memset(inv_size[:], 0.0)
-        for s in LEVELS:
-            cells = slice(first_token[s], first_token[s] + s * s)
-            nc.vector.tensor_scalar_mul(out=inv_size[:, cells], in0=ones[:, cells], scalar1=float(s * s) / POSITIONS)
-        tok = keep.tile([P, MAPS, P], F32)
-        nc.vector.memset(tok[:], 0.0)
-
-        vec_t = psum.tile([P, P], BF16, tag="vec_t")
-        nc.tensor.transpose(vec_t[:], vec_rows[:], ident_bf[:])
-        per_ch = keep.tile([P, 12], F32)
-        nc.vector.tensor_copy(out=per_ch[:], in_=vec_t[:, 0:12])
-        bk_c, gk_c, betak_c, mk_c, vk_c, bv_c = [per_ch[:, 2 * v : 2 * v + 2] for v in range(6)]
-        var_eps = keep.tile([P, 2], F32)
-        nc.vector.tensor_scalar_add(out=var_eps[:], in0=vk_c, scalar1=EPS)
-        std = keep.tile([P, 2], F32)
-        nc.scalar.activation(out=std[:], in_=var_eps[:], func=ACT.Sqrt)
-        inv_std = keep.tile([P, 2], F32)
-        nc.vector.reciprocal(out=inv_std[:], in_=std[:])
-        gain = keep.tile([P, 2], F32)
-        nc.vector.tensor_mul(out=gain[:], in0=inv_std[:], in1=gk_c)
-        centred = keep.tile([P, 2], F32)
-        nc.vector.tensor_sub(out=centred[:], in0=bk_c, in1=mk_c)
-        scaled = keep.tile([P, 2], F32)
-        nc.vector.tensor_mul(out=scaled[:], in0=centred[:], in1=gain[:])
-        shift = keep.tile([P, 2], F32)
-        nc.vector.tensor_add(out=shift[:], in0=scaled[:], in1=betak_c)
-
-        kf_out = out_0[0].rearrange("(m p) h w -> p m (h w)", p=P)
-        row_sums8 = keep.tile([P, MAPS, HEIGHT * 8], F32)
-
-        for band in range(BANDS):
+        def regroup_and_quantise(band):
             grouped = keep.tile([P, GROUPS, BAND, PACK], BF16, name="grouped_%d" % band, align_bytes=64)
             for g in range(GROUPS):
-                src = raw[g, band][:].rearrange("p t (c i) -> p c t i", i=4)
-                dst = grouped[:, g].rearrange("p (c i) t -> p c t i", i=4)
-                nc.vector.tensor_copy(out=dst[:, 0:VECTOR_BLOCKS], in_=src[:, 0:VECTOR_BLOCKS])
-                nc.scalar.copy(out=dst[:, VECTOR_BLOCKS:], in_=src[:, VECTOR_BLOCKS:])
-            codes = keep.tile([P, GROUPS * BAND], U32, name="codes_%d" % band, align_bytes=64)
-            scales = keep.tile([P, GROUPS * BAND], U8, name="scales_%d" % band, align_bytes=64)
+                nc.vector.tensor_copy(
+                    out=grouped[:, g].rearrange("p (c i) t -> p c t i", i=4),
+                    in_=raw[g, band][:].rearrange("p t (c i) -> p c t i", i=4),
+                )
+            codes[band] = keep.tile([P, GROUPS * BAND], U32, name="codes_%d" % band, align_bytes=64)
+            scales[band] = keep.tile([P, GROUPS * BAND], U8, name="scales_%d" % band, align_bytes=64)
             flat = grouped[:].rearrange("p g c t -> p (g c t)")
             for first, width in ((0, 512), (512, 256)):
                 nc.vector.quantize_mx(
-                    out=codes[:, first : first + width].bitcast(FP8X4),
-                    scales=scales[:, first : first + width],
+                    out=codes[band][:, first : first + width].bitcast(FP8X4),
+                    scales=scales[band][:, first : first + width],
                     in_=flat[:, PACK * first : PACK * (first + width)],
                 )
 
-            maps = keep.tile([P, MAPS, BAND], F32, name="maps_%d" % band)
-            for q in range(MAPS):
-                wt, m = divmod(q, 2)
-                acc = psum.tile([P, BAND], F32, tag="acc", bufs=6)
-                for s in range(BAND // SLICE):
+        def project_kf(band):
+            kf[band] = keep.tile([P, HALVES, BAND], F32, name="kf_%d" % band)
+            for m in range(HALVES):
+                acc = psum.tile([P, BAND], F32, tag="kf", bufs=2)
+                for s in range(SLICES):
                     for g in range(GROUPS):
                         cols = slice(g * BAND + s * SLICE, g * BAND + (s + 1) * SLICE)
                         nc.tensor.matmul_mx(
                             out=acc[:, s * SLICE : (s + 1) * SLICE],
-                            lhsT=w_words[:, wt, g, 2 * P * m : 2 * P * (m + 1)].bitcast(FP4X4),
-                            lhsT_scale=w_planes[:, wt, g, P * m : P * (m + 1)],
-                            rhs=codes[:, cols].bitcast(FP8X4),
-                            rhs_scale=scales[:, cols],
+                            lhsT=w_words[:, 0, g, 2 * P * m : 2 * P * (m + 1)].bitcast(FP4X4),
+                            lhsT_scale=w_planes[:, 0, g, P * m : P * (m + 1)],
+                            rhs=codes[band][:, cols].bitcast(FP8X4),
+                            rhs_scale=scales[band][:, cols],
                             start=(g == 0),
                             stop=(g == GROUPS - 1),
                         )
-                if wt == 0:
-                    nc.scalar.activation(
-                        out=maps[:, q, :], in_=acc[:], func=ACT.Relu, bias=shift[:, m : m + 1], scale=gain[:, m : m + 1]
-                    )
-                else:
-                    nc.scalar.activation(out=maps[:, q, :], in_=acc[:], func=ACT.Identity, bias=bv_c[:, m : m + 1])
-            nc.sync.dma_start(out=kf_out[:, :, band * BAND : (band + 1) * BAND], in_=maps[:, 0:2, :])
+                nc.scalar.activation(
+                    out=kf[band][:, m, :], in_=acc[:], func=ACT.Relu, bias=shift[:, m : m + 1], scale=gain[:, m : m + 1]
+                )
+            nc.sync.dma_start(out=kf_out[:, :, band * BAND : (band + 1) * BAND], in_=kf[band][:])
 
-            halves = maps[:].rearrange("p q (n two) -> p q n two", two=2)
-            pair = keep.tile([P, MAPS, BAND // 2], F32, name="pair_%d" % band)
+        def project_val(band):
+            for s in range(SLICES):
+                val_acc = psum.tile([P, HALVES * P], F32, tag="val", bufs=3)
+                for m in range(HALVES):
+                    for g in range(GROUPS):
+                        cols = slice(g * BAND + s * SLICE, g * BAND + (s + 1) * SLICE)
+                        nc.tensor.matmul_mx(
+                            out=val_acc[:, m * P : (m + 1) * P],
+                            lhsT=codes[band][:, cols].bitcast(FP8X4),
+                            lhsT_scale=scales[band][:, cols],
+                            rhs=w_words[:, 1, g, 2 * P * m : 2 * P * (m + 1)].bitcast(FP4X4),
+                            rhs_scale=w_planes[:, 1, g, P * m : P * (m + 1)],
+                            start=(g == 0),
+                            stop=(g == GROUPS - 1),
+                        )
+                block = band * SLICES + s
+                val[block] = keep.tile([P, HALVES * P], F32, name="val_%d" % block)
+                nc.scalar.copy(out=val[block][:], in_=val_acc[:])
+
+        def pool_val(band):
+            for block in range(band * SLICES, (band + 1) * SLICES):
+                nc.tensor.matmul(
+                    out=value_acc[:], lhsT=pool_mat[:, block, :], rhs=val[block][:], start=False, stop=(block == BLOCKS - 1)
+                )
+
+        def pool_kf(band):
+            halves = kf[band][:].rearrange("p q (n two) -> p q n two", two=2)
+            pair = keep.tile([P, HALVES, BAND // 2], F32, name="pair_%d" % band)
             nc.vector.tensor_tensor(out=pair[:], in0=halves[:, :, :, 0], in1=halves[:, :, :, 1], op=ADD)
+            nc.vector.tensor_reduce(
+                out=row_sums8[:, :, 64 * band : 64 * (band + 1)],
+                in_=pair[:].rearrange("p q (n j) -> p q n j", j=3),
+                axis=AXIS.X,
+                op=ADD,
+            )
             for a in (2 * band, 2 * band + 1):
                 rows = pair[:, :, 96 * (a - 2 * band) : 96 * (a - 2 * band + 1)]
                 nc.vector.tensor_reduce(
@@ -159,12 +141,6 @@ def tile_apnb_pa_kernel(
                     axis=AXIS.XY,
                     op=ADD,
                 )
-            nc.vector.tensor_reduce(
-                out=row_sums8[:, :, 64 * band : 64 * (band + 1)],
-                in_=pair[:].rearrange("p q (n j) -> p q n j", j=3),
-                axis=AXIS.X,
-                op=ADD,
-            )
             a_done, a_new = (BAND_ROWS * band) // 3, (BAND_ROWS * (band + 1)) // 3
             nc.vector.tensor_reduce(
                 out=tok[:, :, first_token[8] + 8 * a_done : first_token[8] + 8 * a_new].rearrange(
@@ -182,16 +158,109 @@ def tile_apnb_pa_kernel(
                 axis=AXIS.XY,
                 op=ADD,
             )
-        nc.vector.tensor_reduce(out=tok[:, :, 0], in_=tok[:, :, 1:10], axis=AXIS.X, op=ADD)
 
-        means = keep.tile([P, MAPS, P], F32)
-        both = inv_size[:].unsqueeze(1).to_broadcast([P, 2, P])
-        nc.vector.tensor_tensor(out=means[:, 2:4, :], in0=tok[:, 2:4, :], in1=both, op=MULT)
-        nc.vector.tensor_tensor(out=means[:, 0:2, :], in0=tok[:, 0:2, :], in1=both, op=MULT)
-        value_t = psum.tile([P, 2 * P], F32, tag="value_t")
-        for m in range(2):
-            nc.tensor.transpose(value_t[:, m * P : (m + 1) * P], means[:, 2 + m, :], ident[:])
-        value_sb = keep.tile([P, 2 * P], F32)
-        nc.scalar.copy(out=value_sb[:], in_=value_t[:])
+        cell_of = keep.tile([P, POSITIONS], F32)
+        nc.vector.memset(cell_of[:], 0.0)
+        w_words = keep.tile([P, 2, GROUPS, 4 * P], U8, align_bytes=64)
+        w_planes = keep.tile([P, 2, GROUPS, 2 * P], U8, align_bytes=64)
+        nc.vector.memset(w_planes[:].bitcast(I32), 0)
+        vec_rows = keep.tile([P, P], BF16)
+        nc.vector.memset(vec_rows[:], 0.0)
+        bv_row = keep.tile([P, HALVES * P], BF16)
+        nc.vector.memset(bv_row[:], 0.0)
+
+        load_band(0)
+        for wt, (words, scales_in) in enumerate(((Wk_words, Wk_scales), (Wv_words, Wv_scales))):
+            for quad in range(4):
+                nc.sync.dma_start(
+                    out=w_planes[32 * quad : 32 * quad + 4, wt].bitcast(I32),
+                    in_=scales_in.bitcast(I32)[:, 4 * quad : 4 * quad + 4, :].rearrange("g r n -> r g n"),
+                )
+            nc.sync.dma_start(out=w_words[:, wt].bitcast(I32), in_=words.bitcast(I32).rearrange("g p n -> p g n"))
+        load_band(1)
+        load_band(2)
+        for v, vec in enumerate((bk, gk, betak, mk, vk)):
+            nc.scalar.dma_start(out=vec_rows[2 * v : 2 * v + 2, :], in_=vec.rearrange("(m c) -> m c", m=2))
+        nc.scalar.dma_start(out=bv_row[0:1, :], in_=bv.rearrange("(o c) -> o c", o=1))
+
+        ident = keep.tile([P, P], F32)
+        make_identity(nc, ident[:])
+        for s in LEVELS:
+            nc.gpsimd.affine_select(
+                out=cell_of[:],
+                in_=cell_of[:],
+                compare_op=NOT_EQUAL,
+                fill=float(s * s) / 128.0,
+                base=-first_token[s],
+                pattern=[[-s, s], [0, HEIGHT // s], [-1, s], [0, WIDTH // s]],
+                channel_multiplier=1,
+            )
+        ones = keep.tile([P, TOKENS], F32)
+        nc.vector.memset(ones[:], 1.0)
+        warm = keep.tile([P, 1], F32)
+        nc.scalar.activation(out=warm[:], in_=ones[:, 0:1], func=ACT.Sqrt)
+        nines_bf = keep.tile([P, P], BF16)
+        nc.vector.memset(nines_bf[:], 9.0)
+        inv_size = keep.tile([P, TOKENS], F32)
+        for s in LEVELS:
+            cells = slice(first_token[s], first_token[s] + s * s)
+            nc.vector.tensor_scalar_mul(out=inv_size[:, cells], in0=ones[:, cells], scalar1=float(s * s) / POSITIONS)
+        ident_bf = keep.tile([P, P], BF16)
+        nc.vector.tensor_copy(out=ident_bf[:], in_=ident[:])
+        row_sums8 = keep.tile([P, HALVES, HEIGHT * 8], F32)
+        tok = keep.tile([P, HALVES, TOKENS], F32)
+
+        regroup_and_quantise(0)
+
+        vec_t = psum.tile([P, P], BF16, tag="setup", bufs=2)
+        nc.tensor.transpose(vec_t[:], vec_rows[:], ident_bf[:])
+        per_ch = keep.tile([P, 10], F32)
+        nc.vector.tensor_copy(out=per_ch[:], in_=vec_t[:, 0:10])
+        bk_c, gk_c, betak_c, mk_c, vk_c = [per_ch[:, 2 * v : 2 * v + 2] for v in range(5)]
+        var_eps = keep.tile([P, 2], F32)
+        nc.vector.tensor_scalar_add(out=var_eps[:], in0=vk_c, scalar1=EPS)
+        std = keep.tile([P, 2], F32)
+        nc.scalar.activation(out=std[:], in_=var_eps[:], func=ACT.Sqrt)
+        centred = keep.tile([P, 2], F32)
+        nc.vector.tensor_sub(out=centred[:], in0=bk_c, in1=mk_c)
+        inv_std = keep.tile([P, 2], F32)
+        nc.vector.reciprocal(out=inv_std[:], in_=std[:])
+        gain = keep.tile([P, 2], F32)
+        nc.vector.tensor_mul(out=gain[:], in0=inv_std[:], in1=gk_c)
+        scaled = keep.tile([P, 2], F32)
+        nc.vector.tensor_mul(out=scaled[:], in0=centred[:], in1=gain[:])
+        shift = keep.tile([P, 2], F32)
+        nc.vector.tensor_add(out=shift[:], in0=scaled[:], in1=betak_c)
+
+        value_acc = psum.tile([P, HALVES * P], F32, tag="value")
+        nc.tensor.matmul(out=value_acc[:], lhsT=nines_bf[:], rhs=bv_row[:], start=True, stop=False)
+
+        regroup_and_quantise(1)
+
+        pool_mat = keep.tile([P, BLOCKS, P], F32)
+        for band in range(BANDS):
+            project_kf(band)
+            project_val(band)
+            if band == 0:
+                for first in range(0, BLOCKS, 4):
+                    count = min(4, BLOCKS - first)
+                    flipped = psum.tile([P, 4, P], F32, tag="setup", bufs=2)
+                    for j in range(count):
+                        nc.tensor.transpose(flipped[:, j, :], cell_of[:, (first + j) * P : (first + j + 1) * P], ident[:])
+                    nc.scalar.copy(out=pool_mat[:, first : first + count, :], in_=flipped[:, 0:count, :])
+            else:
+                pool_val(band - 1)
+            if band + AHEAD < BANDS:
+                regroup_and_quantise(band + AHEAD)
+            pool_kf(band)
+        pool_val(BANDS - 1)
+
+        value_sb = keep.tile([P, HALVES * P], F32)
+        nc.scalar.mul(out=value_sb[:], in_=value_acc[:], mul=1.0 / 9.0)
         nc.sync.dma_start(out=out_2[0], in_=value_sb[0:TOKENS, :])
-        nc.sync.dma_start(out=out_1[0].rearrange("(m p) t -> p m t", p=P), in_=means[:, 0:2, 0:TOKENS])
+        nc.vector.tensor_reduce(out=tok[:, :, 0], in_=tok[:, :, 1:10], axis=AXIS.X, op=ADD)
+        keyp = keep.tile([P, HALVES, TOKENS], F32)
+        nc.vector.tensor_tensor(
+            out=keyp[:], in0=tok[:], in1=inv_size[:].unsqueeze(1).to_broadcast([P, HALVES, TOKENS]), op=MULT
+        )
+        nc.sync.dma_start(out=out_1[0].rearrange("(m p) t -> p m t", p=P), in_=keyp[:])

@@ -12,7 +12,6 @@ FP8X4 = mybir.dt.float8_e4m3fn_x4
 FP4X4 = mybir.dt.float4_e2m1fn_x4
 ADD = mybir.AluOpType.add
 MULT = mybir.AluOpType.mult
-NOT_EQUAL = mybir.AluOpType.not_equal
 ACT = mybir.ActivationFunctionType
 AXIS = mybir.AxisListType
 
@@ -159,8 +158,6 @@ def tile_apnb_pa_kernel(
                 op=ADD,
             )
 
-        cell_of = keep.tile([P, POSITIONS], F32)
-        nc.vector.memset(cell_of[:], 0.0)
         w_words = keep.tile([P, 2, GROUPS, 4 * P], U8, align_bytes=64)
         w_planes = keep.tile([P, 2, GROUPS, 2 * P], U8, align_bytes=64)
         nc.vector.memset(w_planes[:].bitcast(I32), 0)
@@ -168,6 +165,10 @@ def tile_apnb_pa_kernel(
         nc.vector.memset(vec_rows[:], 0.0)
         bv_row = keep.tile([P, HALVES * P], BF16)
         nc.vector.memset(bv_row[:], 0.0)
+        one = keep.tile([P, 1], F32)
+        nc.vector.memset(one[:], 1.0)
+        pool_mat = keep.tile([P, BLOCKS, P], F32)
+        nc.vector.memset(pool_mat[:], 0.0)
 
         load_band(0)
         for wt, (words, scales_in) in enumerate(((Wk_words, Wk_scales), (Wv_words, Wv_scales))):
@@ -185,26 +186,49 @@ def tile_apnb_pa_kernel(
 
         ident = keep.tile([P, P], F32)
         make_identity(nc, ident[:])
-        for s in LEVELS:
-            nc.gpsimd.affine_select(
-                out=cell_of[:],
-                in_=cell_of[:],
-                compare_op=NOT_EQUAL,
-                fill=float(s * s) / 128.0,
-                base=-first_token[s],
-                pattern=[[-s, s], [0, HEIGHT // s], [-1, s], [0, WIDTH // s]],
-                channel_multiplier=1,
-            )
-        ones = keep.tile([P, TOKENS], F32)
-        nc.vector.memset(ones[:], 1.0)
         warm = keep.tile([P, 1], F32)
-        nc.scalar.activation(out=warm[:], in_=ones[:, 0:1], func=ACT.Sqrt)
+        nc.scalar.activation(out=warm[:], in_=one[:], func=ACT.Sqrt)
+
+        where = keep.tile([P, POSITIONS], BF16)
+        nc.vector.tensor_tensor(
+            out=where[:].rearrange("p (h c two) -> p h c two", h=HEIGHT, two=2),
+            in0=ident[:, 0:HEIGHT].unsqueeze(2).unsqueeze(3).to_broadcast([P, HEIGHT, WIDTH // 2, 2]),
+            in1=ident[:, HEIGHT : 2 * HEIGHT].unsqueeze(1).unsqueeze(3).to_broadcast([P, HEIGHT, WIDTH // 2, 2]),
+            op=ADD,
+        )
+        which = keep.tile([P, TOKENS], BF16)
+        for s in LEVELS:
+            member = keep.tile([P, 2, s], F32, name="member_%d" % s)
+            nc.vector.tensor_reduce(
+                out=member[:],
+                in_=ident[:, 0 : 2 * HEIGHT].rearrange("p (part a i) -> p part a i", part=2, a=s),
+                axis=AXIS.X,
+                op=ADD,
+            )
+            nc.vector.scalar_tensor_tensor(
+                out=which[:, first_token[s] : first_token[s] + s * s].rearrange("p (a b) -> p a b", b=s),
+                in0=member[:, 0, :].unsqueeze(2).to_broadcast([P, s, s]),
+                scalar=float(s * s) / 128.0,
+                in1=member[:, 1, :].unsqueeze(1).to_broadcast([P, s, s]),
+                op0=MULT,
+                op1=ADD,
+            )
+        for first in range(0, BLOCKS, 4):
+            count = min(4, BLOCKS - first)
+            hits = psum.tile([P, 4, TOKENS], F32, tag="setup", bufs=2)
+            for j in range(count):
+                nc.tensor.matmul(
+                    out=hits[:, j, :],
+                    lhsT=where[:, (first + j) * P : (first + j + 1) * P],
+                    rhs=which[:],
+                    start=True,
+                    stop=True,
+                )
+            nc.scalar.activation(
+                out=pool_mat[:, first : first + count, 0:TOKENS], in_=hits[:, 0:count, :], func=ACT.Relu, bias=-1.0
+            )
         nines_bf = keep.tile([P, P], BF16)
         nc.vector.memset(nines_bf[:], 9.0)
-        inv_size = keep.tile([P, TOKENS], F32)
-        for s in LEVELS:
-            cells = slice(first_token[s], first_token[s] + s * s)
-            nc.vector.tensor_scalar_mul(out=inv_size[:, cells], in0=ones[:, cells], scalar1=float(s * s) / POSITIONS)
         ident_bf = keep.tile([P, P], BF16)
         nc.vector.tensor_copy(out=ident_bf[:], in_=ident[:])
         row_sums8 = keep.tile([P, HALVES, HEIGHT * 8], F32)
@@ -232,28 +256,25 @@ def tile_apnb_pa_kernel(
         shift = keep.tile([P, 2], F32)
         nc.vector.tensor_add(out=shift[:], in0=scaled[:], in1=betak_c)
 
+        ones = keep.tile([P, TOKENS], F32)
+        nc.vector.memset(ones[:], 1.0)
+        inv_size = keep.tile([P, TOKENS], F32)
+        for s in LEVELS:
+            cells = slice(first_token[s], first_token[s] + s * s)
+            nc.vector.tensor_scalar_mul(out=inv_size[:, cells], in0=ones[:, cells], scalar1=float(s * s) / POSITIONS)
+
         value_acc = psum.tile([P, HALVES * P], F32, tag="value")
         nc.tensor.matmul(out=value_acc[:], lhsT=nines_bf[:], rhs=bv_row[:], start=True, stop=False)
 
         regroup_and_quantise(1)
 
-        pool_mat = keep.tile([P, BLOCKS, P], F32)
         for band in range(BANDS):
             project_kf(band)
             project_val(band)
-            if band == 0:
-                for first in range(0, BLOCKS, 4):
-                    count = min(4, BLOCKS - first)
-                    flipped = psum.tile([P, 4, P], F32, tag="setup", bufs=2)
-                    for j in range(count):
-                        nc.tensor.transpose(flipped[:, j, :], cell_of[:, (first + j) * P : (first + j + 1) * P], ident[:])
-                    nc.scalar.copy(out=pool_mat[:, first : first + count, :], in_=flipped[:, 0:count, :])
-            else:
-                pool_val(band - 1)
+            pool_val(band)
             if band + AHEAD < BANDS:
                 regroup_and_quantise(band + AHEAD)
             pool_kf(band)
-        pool_val(BANDS - 1)
 
         value_sb = keep.tile([P, HALVES * P], F32)
         nc.scalar.mul(out=value_sb[:], in_=value_acc[:], mul=1.0 / 9.0)

@@ -54,10 +54,17 @@ def tile_apnb_pa_kernel(
         kf = {}
         val = {}
 
-        def load_band(band):
-            for g in range(GROUPS):
-                raw[g, band] = keep.tile([P, PACK, BAND], BF16, name="raw_%d_%d" % (g, band))
-                nc.sync.dma_start(out=raw[g, band][:], in_=x_rows[g, :, :, band * BAND : (band + 1) * BAND])
+        def load_x(g, band):
+            raw[g, band] = keep.tile([P, PACK, BAND], BF16, name="raw_%d_%d" % (g, band))
+            nc.sync.dma_start(out=raw[g, band][:], in_=x_rows[g, :, :, band * BAND : (band + 1) * BAND])
+
+        def load_weight(wt, words, scales_in):
+            for quad in range(4):
+                nc.sync.dma_start(
+                    out=w_planes[32 * quad : 32 * quad + 4, wt].bitcast(I32),
+                    in_=scales_in.bitcast(I32)[:, 4 * quad : 4 * quad + 4, :].rearrange("g r n -> r g n"),
+                )
+            nc.sync.dma_start(out=w_words[:, wt].bitcast(I32), in_=words.bitcast(I32).rearrange("g p n -> p g n"))
 
         def regroup_and_quantise(band):
             grouped = keep.tile([P, GROUPS, BAND, PACK], BF16, name="grouped_%d" % band, align_bytes=64)
@@ -158,36 +165,44 @@ def tile_apnb_pa_kernel(
                 op=ADD,
             )
 
-        w_words = keep.tile([P, 2, GROUPS, 4 * P], U8, align_bytes=64)
-        w_planes = keep.tile([P, 2, GROUPS, 2 * P], U8, align_bytes=64)
-        nc.vector.memset(w_planes[:].bitcast(I32), 0)
         vec_rows = keep.tile([P, P], BF16)
         nc.vector.memset(vec_rows[:], 0.0)
         bv_row = keep.tile([P, HALVES * P], BF16)
         nc.vector.memset(bv_row[:], 0.0)
+        w_words = keep.tile([P, 2, GROUPS, 4 * P], U8, align_bytes=64)
+        w_planes = keep.tile([P, 2, GROUPS, 2 * P], U8, align_bytes=64)
+        nc.vector.memset(w_planes[:].bitcast(I32), 0)
         one = keep.tile([P, 1], F32)
         nc.vector.memset(one[:], 1.0)
         pool_mat = keep.tile([P, BLOCKS, P], F32)
         nc.vector.memset(pool_mat[:], 0.0)
+        nines_bf = keep.tile([P, P], BF16)
+        nc.vector.memset(nines_bf[:], 9.0)
 
-        load_band(0)
-        for wt, (words, scales_in) in enumerate(((Wk_words, Wk_scales), (Wv_words, Wv_scales))):
-            for quad in range(4):
-                nc.sync.dma_start(
-                    out=w_planes[32 * quad : 32 * quad + 4, wt].bitcast(I32),
-                    in_=scales_in.bitcast(I32)[:, 4 * quad : 4 * quad + 4, :].rearrange("g r n -> r g n"),
-                )
-            nc.sync.dma_start(out=w_words[:, wt].bitcast(I32), in_=words.bitcast(I32).rearrange("g p n -> p g n"))
-        load_band(1)
-        load_band(2)
         for v, vec in enumerate((bk, gk, betak, mk, vk)):
             nc.scalar.dma_start(out=vec_rows[2 * v : 2 * v + 2, :], in_=vec.rearrange("(m c) -> m c", m=2))
         nc.scalar.dma_start(out=bv_row[0:1, :], in_=bv.rearrange("(o c) -> o c", o=1))
+        load_x(0, 0)
+        load_x(1, 0)
+        load_weight(0, Wk_words, Wk_scales)
+        load_x(0, 1)
+        load_weight(1, Wv_words, Wv_scales)
+        load_x(1, 1)
+        load_x(0, 2)
+        load_x(1, 2)
 
         ident = keep.tile([P, P], F32)
         make_identity(nc, ident[:])
+        ones = keep.tile([P, TOKENS], F32)
+        nc.gpsimd.memset(ones[:], 1.0)
+        inv_size = keep.tile([P, TOKENS], F32)
+        for s in LEVELS:
+            cells = slice(first_token[s], first_token[s] + s * s)
+            nc.gpsimd.tensor_scalar_mul(out=inv_size[:, cells], in0=ones[:, cells], scalar1=float(s * s) / POSITIONS)
         warm = keep.tile([P, 1], F32)
         nc.scalar.activation(out=warm[:], in_=one[:], func=ACT.Sqrt)
+        ident_bf = keep.tile([P, P], BF16)
+        nc.vector.tensor_copy(out=ident_bf[:], in_=ident[:])
 
         where = keep.tile([P, POSITIONS], BF16)
         nc.vector.tensor_tensor(
@@ -213,28 +228,6 @@ def tile_apnb_pa_kernel(
                 op0=MULT,
                 op1=ADD,
             )
-        for first in range(0, BLOCKS, 4):
-            count = min(4, BLOCKS - first)
-            hits = psum.tile([P, 4, TOKENS], F32, tag="setup", bufs=2)
-            for j in range(count):
-                nc.tensor.matmul(
-                    out=hits[:, j, :],
-                    lhsT=where[:, (first + j) * P : (first + j + 1) * P],
-                    rhs=which[:],
-                    start=True,
-                    stop=True,
-                )
-            nc.scalar.activation(
-                out=pool_mat[:, first : first + count, 0:TOKENS], in_=hits[:, 0:count, :], func=ACT.Relu, bias=-1.0
-            )
-        nines_bf = keep.tile([P, P], BF16)
-        nc.vector.memset(nines_bf[:], 9.0)
-        ident_bf = keep.tile([P, P], BF16)
-        nc.vector.tensor_copy(out=ident_bf[:], in_=ident[:])
-        row_sums8 = keep.tile([P, HALVES, HEIGHT * 8], F32)
-        tok = keep.tile([P, HALVES, TOKENS], F32)
-
-        regroup_and_quantise(0)
 
         vec_t = psum.tile([P, P], BF16, tag="setup", bufs=2)
         nc.tensor.transpose(vec_t[:], vec_rows[:], ident_bf[:])
@@ -256,17 +249,28 @@ def tile_apnb_pa_kernel(
         shift = keep.tile([P, 2], F32)
         nc.vector.tensor_add(out=shift[:], in0=scaled[:], in1=betak_c)
 
-        ones = keep.tile([P, TOKENS], F32)
-        nc.vector.memset(ones[:], 1.0)
-        inv_size = keep.tile([P, TOKENS], F32)
-        for s in LEVELS:
-            cells = slice(first_token[s], first_token[s] + s * s)
-            nc.vector.tensor_scalar_mul(out=inv_size[:, cells], in0=ones[:, cells], scalar1=float(s * s) / POSITIONS)
-
         value_acc = psum.tile([P, HALVES * P], F32, tag="value")
         nc.tensor.matmul(out=value_acc[:], lhsT=nines_bf[:], rhs=bv_row[:], start=True, stop=False)
 
-        regroup_and_quantise(1)
+        for first in range(0, BLOCKS, 4):
+            count = min(4, BLOCKS - first)
+            hits = psum.tile([P, 4, TOKENS], F32, tag="setup", bufs=2)
+            for j in range(count):
+                nc.tensor.matmul(
+                    out=hits[:, j, :],
+                    lhsT=where[:, (first + j) * P : (first + j + 1) * P],
+                    rhs=which[:],
+                    start=True,
+                    stop=True,
+                )
+            nc.scalar.activation(
+                out=pool_mat[:, first : first + count, 0:TOKENS], in_=hits[:, 0:count, :], func=ACT.Relu, bias=-1.0
+            )
+
+        row_sums8 = keep.tile([P, HALVES, HEIGHT * 8], F32)
+        tok = keep.tile([P, HALVES, TOKENS], F32)
+        for band in range(AHEAD):
+            regroup_and_quantise(band)
 
         for band in range(BANDS):
             project_kf(band)

@@ -12,6 +12,7 @@ FP8X4 = mybir.dt.float8_e4m3fn_x4
 FP4X4 = mybir.dt.float4_e2m1fn_x4
 ADD = mybir.AluOpType.add
 MULT = mybir.AluOpType.mult
+SUBTRACT = mybir.AluOpType.subtract
 ACT = mybir.ActivationFunctionType
 AXIS = mybir.AxisListType
 
@@ -31,7 +32,6 @@ HALVES = 2
 LEVELS = (1, 3, 6, 8)
 TOKENS = 110
 EPS = 1e-5
-AHEAD = 2
 
 FLOPS = 2 * 512 * 1024 * POSITIONS
 
@@ -54,17 +54,10 @@ def tile_apnb_pa_kernel(
         kf = {}
         val = {}
 
-        def load_x(g, band):
-            raw[g, band] = keep.tile([P, PACK, BAND], BF16, name="raw_%d_%d" % (g, band))
-            nc.sync.dma_start(out=raw[g, band][:], in_=x_rows[g, :, :, band * BAND : (band + 1) * BAND])
-
-        def load_weight(wt, words, scales_in):
-            for quad in range(4):
-                nc.sync.dma_start(
-                    out=w_planes[32 * quad : 32 * quad + 4, wt].bitcast(I32),
-                    in_=scales_in.bitcast(I32)[:, 4 * quad : 4 * quad + 4, :].rearrange("g r n -> r g n"),
-                )
-            nc.sync.dma_start(out=w_words[:, wt].bitcast(I32), in_=words.bitcast(I32).rearrange("g p n -> p g n"))
+        def load_band(band):
+            for g in range(GROUPS):
+                raw[g, band] = keep.tile([P, PACK, BAND], BF16, name="raw_%d_%d" % (g, band))
+                nc.sync.dma_start(out=raw[g, band][:], in_=x_rows[g, :, :, band * BAND : (band + 1) * BAND])
 
         def regroup_and_quantise(band):
             grouped = keep.tile([P, GROUPS, BAND, PACK], BF16, name="grouped_%d" % band, align_bytes=64)
@@ -86,7 +79,7 @@ def tile_apnb_pa_kernel(
         def project_kf(band):
             kf[band] = keep.tile([P, HALVES, BAND], F32, name="kf_%d" % band)
             for m in range(HALVES):
-                acc = psum.tile([P, BAND], F32, tag="kf", bufs=2)
+                acc = psum.tile([P, BAND], F32, tag="kf", bufs=4)
                 for s in range(SLICES):
                     for g in range(GROUPS):
                         cols = slice(g * BAND + s * SLICE, g * BAND + (s + 1) * SLICE)
@@ -126,7 +119,7 @@ def tile_apnb_pa_kernel(
         def pool_val(band):
             for block in range(band * SLICES, (band + 1) * SLICES):
                 nc.tensor.matmul(
-                    out=value_acc[:], lhsT=pool_mat[:, block, :], rhs=val[block][:], start=False, stop=(block == BLOCKS - 1)
+                    out=value_acc[:], lhsT=pool_mat[:, block, :], rhs=val[block][:], start=(block == 0), stop=False
                 )
 
         def pool_kf(band):
@@ -165,44 +158,36 @@ def tile_apnb_pa_kernel(
                 op=ADD,
             )
 
+        w_words = keep.tile([P, 2, GROUPS, 4 * P], U8, align_bytes=64)
+        w_planes = keep.tile([P, 2, GROUPS, 2 * P], U8, align_bytes=64)
+        nc.vector.memset(w_planes[:].bitcast(I32), 0)
         vec_rows = keep.tile([P, P], BF16)
         nc.vector.memset(vec_rows[:], 0.0)
         bv_row = keep.tile([P, HALVES * P], BF16)
         nc.vector.memset(bv_row[:], 0.0)
-        w_words = keep.tile([P, 2, GROUPS, 4 * P], U8, align_bytes=64)
-        w_planes = keep.tile([P, 2, GROUPS, 2 * P], U8, align_bytes=64)
-        nc.vector.memset(w_planes[:].bitcast(I32), 0)
         one = keep.tile([P, 1], F32)
         nc.vector.memset(one[:], 1.0)
         pool_mat = keep.tile([P, BLOCKS, P], F32)
         nc.vector.memset(pool_mat[:], 0.0)
-        nines_bf = keep.tile([P, P], BF16)
-        nc.vector.memset(nines_bf[:], 9.0)
 
+        load_band(0)
+        for wt, words, scales_in in ((1, Wv_words, Wv_scales), (0, Wk_words, Wk_scales)):
+            for quad in range(4):
+                nc.sync.dma_start(
+                    out=w_planes[32 * quad : 32 * quad + 4, wt].bitcast(I32),
+                    in_=scales_in.bitcast(I32)[:, 4 * quad : 4 * quad + 4, :].rearrange("g r n -> r g n"),
+                )
+            nc.sync.dma_start(out=w_words[:, wt].bitcast(I32), in_=words.bitcast(I32).rearrange("g p n -> p g n"))
+        load_band(1)
+        load_band(2)
         for v, vec in enumerate((bk, gk, betak, mk, vk)):
             nc.scalar.dma_start(out=vec_rows[2 * v : 2 * v + 2, :], in_=vec.rearrange("(m c) -> m c", m=2))
         nc.scalar.dma_start(out=bv_row[0:1, :], in_=bv.rearrange("(o c) -> o c", o=1))
-        load_x(0, 0)
-        load_x(1, 0)
-        load_weight(0, Wk_words, Wk_scales)
-        load_x(0, 1)
-        load_weight(1, Wv_words, Wv_scales)
-        load_x(1, 1)
-        load_x(0, 2)
-        load_x(1, 2)
 
         ident = keep.tile([P, P], F32)
         make_identity(nc, ident[:])
-        ones = keep.tile([P, TOKENS], F32)
-        nc.gpsimd.memset(ones[:], 1.0)
-        inv_size = keep.tile([P, TOKENS], F32)
-        for s in LEVELS:
-            cells = slice(first_token[s], first_token[s] + s * s)
-            nc.gpsimd.tensor_scalar_mul(out=inv_size[:, cells], in0=ones[:, cells], scalar1=float(s * s) / POSITIONS)
         warm = keep.tile([P, 1], F32)
-        nc.scalar.activation(out=warm[:], in_=one[:], func=ACT.Sqrt)
-        ident_bf = keep.tile([P, P], BF16)
-        nc.vector.tensor_copy(out=ident_bf[:], in_=ident[:])
+        nc.scalar.activation(out=warm[:], in_=one[:], func=ACT.Abs_reciprocal_sqrt)
 
         where = keep.tile([P, POSITIONS], BF16)
         nc.vector.tensor_tensor(
@@ -228,57 +213,71 @@ def tile_apnb_pa_kernel(
                 op0=MULT,
                 op1=ADD,
             )
-
-        vec_t = psum.tile([P, P], BF16, tag="setup", bufs=2)
-        nc.tensor.transpose(vec_t[:], vec_rows[:], ident_bf[:])
-        per_ch = keep.tile([P, 10], F32)
-        nc.vector.tensor_copy(out=per_ch[:], in_=vec_t[:, 0:10])
-        bk_c, gk_c, betak_c, mk_c, vk_c = [per_ch[:, 2 * v : 2 * v + 2] for v in range(5)]
-        var_eps = keep.tile([P, 2], F32)
-        nc.vector.tensor_scalar_add(out=var_eps[:], in0=vk_c, scalar1=EPS)
-        std = keep.tile([P, 2], F32)
-        nc.scalar.activation(out=std[:], in_=var_eps[:], func=ACT.Sqrt)
-        centred = keep.tile([P, 2], F32)
-        nc.vector.tensor_sub(out=centred[:], in0=bk_c, in1=mk_c)
-        inv_std = keep.tile([P, 2], F32)
-        nc.vector.reciprocal(out=inv_std[:], in_=std[:])
-        gain = keep.tile([P, 2], F32)
-        nc.vector.tensor_mul(out=gain[:], in0=inv_std[:], in1=gk_c)
-        scaled = keep.tile([P, 2], F32)
-        nc.vector.tensor_mul(out=scaled[:], in0=centred[:], in1=gain[:])
-        shift = keep.tile([P, 2], F32)
-        nc.vector.tensor_add(out=shift[:], in0=scaled[:], in1=betak_c)
-
-        value_acc = psum.tile([P, HALVES * P], F32, tag="value")
-        nc.tensor.matmul(out=value_acc[:], lhsT=nines_bf[:], rhs=bv_row[:], start=True, stop=False)
-
+        hits = {}
         for first in range(0, BLOCKS, 4):
-            count = min(4, BLOCKS - first)
-            hits = psum.tile([P, 4, TOKENS], F32, tag="setup", bufs=2)
-            for j in range(count):
+            hits[first] = psum.tile([P, 4, TOKENS], F32, tag="val", bufs=3, name="hits_%d" % first)
+            for j in range(min(4, BLOCKS - first)):
                 nc.tensor.matmul(
-                    out=hits[:, j, :],
+                    out=hits[first][:, j, :],
                     lhsT=where[:, (first + j) * P : (first + j + 1) * P],
                     rhs=which[:],
                     start=True,
                     stop=True,
                 )
-            nc.scalar.activation(
-                out=pool_mat[:, first : first + count, 0:TOKENS], in_=hits[:, 0:count, :], func=ACT.Relu, bias=-1.0
-            )
-
+        nines_bf = keep.tile([P, P], BF16)
+        nc.vector.memset(nines_bf[:], 9.0)
+        ident_bf = keep.tile([P, P], BF16)
+        nc.vector.tensor_copy(out=ident_bf[:], in_=ident[:])
         row_sums8 = keep.tile([P, HALVES, HEIGHT * 8], F32)
         tok = keep.tile([P, HALVES, TOKENS], F32)
-        for band in range(AHEAD):
-            regroup_and_quantise(band)
 
-        for band in range(BANDS):
-            project_kf(band)
+        regroup_and_quantise(0)
+
+        for first in range(0, BLOCKS, 4):
+            count = min(4, BLOCKS - first)
+            nc.scalar.activation(
+                out=pool_mat[:, first : first + count, 0:TOKENS], in_=hits[first][:, 0:count, :], func=ACT.Relu, bias=-1.0
+            )
+
+        ones = keep.tile([P, TOKENS], F32)
+        nc.gpsimd.memset(ones[:], 1.0)
+        inv_size = keep.tile([P, TOKENS], F32)
+        for s in LEVELS:
+            cells = slice(first_token[s], first_token[s] + s * s)
+            nc.gpsimd.tensor_scalar_mul(out=inv_size[:, cells], in0=ones[:, cells], scalar1=float(s * s) / POSITIONS)
+
+        value_acc = psum.tile([P, HALVES * P], F32, tag="value")
+        regroup_and_quantise(1)
+
+        project_val(0)
+
+        vec_t = psum.tile([P, P], BF16, tag="kf", bufs=4)
+        nc.tensor.transpose(vec_t[:], vec_rows[:], ident_bf[:])
+        per_ch = keep.tile([P, 10], F32)
+        nc.scalar.copy(out=per_ch[:], in_=vec_t[:, 0:10])
+        bk_c, gk_c, betak_c, mk_c, vk_c = [per_ch[:, 2 * v : 2 * v + 2] for v in range(5)]
+        inv_std = keep.tile([P, 2], F32)
+        nc.scalar.activation(out=inv_std[:], in_=vk_c, func=ACT.Abs_reciprocal_sqrt, bias=EPS)
+        centred = keep.tile([P, 2], F32)
+        nc.gpsimd.tensor_tensor(out=centred[:], in0=bk_c, in1=mk_c, op=SUBTRACT)
+        gain = keep.tile([P, 2], F32)
+        nc.gpsimd.tensor_tensor(out=gain[:], in0=inv_std[:], in1=gk_c, op=MULT)
+        scaled = keep.tile([P, 2], F32)
+        nc.gpsimd.tensor_tensor(out=scaled[:], in0=centred[:], in1=gain[:], op=MULT)
+        shift = keep.tile([P, 2], F32)
+        nc.gpsimd.tensor_tensor(out=shift[:], in0=scaled[:], in1=betak_c, op=ADD)
+
+        project_kf(0)
+        for band in range(1, BANDS):
+            if band + 1 < BANDS:
+                regroup_and_quantise(band + 1)
             project_val(band)
-            pool_val(band)
-            if band + AHEAD < BANDS:
-                regroup_and_quantise(band + AHEAD)
-            pool_kf(band)
+            project_kf(band)
+            pool_val(band - 1)
+            pool_kf(band - 1)
+        pool_val(BANDS - 1)
+        nc.tensor.matmul(out=value_acc[:], lhsT=nines_bf[:], rhs=bv_row[:], start=False, stop=True)
+        pool_kf(BANDS - 1)
 
         value_sb = keep.tile([P, HALVES * P], F32)
         nc.scalar.mul(out=value_sb[:], in_=value_acc[:], mul=1.0 / 9.0)

@@ -259,13 +259,13 @@ def tile_apnb_pa_kernel(
         inv_std = keep.tile([P, 2], F32)
         nc.scalar.activation(out=inv_std[:], in_=vk_c, func=ACT.Abs_reciprocal_sqrt, bias=EPS)
         centred = keep.tile([P, 2], F32)
-        nc.gpsimd.tensor_tensor(out=centred[:], in0=bk_c, in1=mk_c, op=SUBTRACT)
+        nc.vector.tensor_tensor(out=centred[:], in0=bk_c, in1=mk_c, op=SUBTRACT)
         gain = keep.tile([P, 2], F32)
-        nc.gpsimd.tensor_tensor(out=gain[:], in0=inv_std[:], in1=gk_c, op=MULT)
+        nc.vector.tensor_tensor(out=gain[:], in0=inv_std[:], in1=gk_c, op=MULT)
         scaled = keep.tile([P, 2], F32)
-        nc.gpsimd.tensor_tensor(out=scaled[:], in0=centred[:], in1=gain[:], op=MULT)
+        nc.vector.tensor_tensor(out=scaled[:], in0=centred[:], in1=gain[:], op=MULT)
         shift = keep.tile([P, 2], F32)
-        nc.gpsimd.tensor_tensor(out=shift[:], in0=scaled[:], in1=betak_c, op=ADD)
+        nc.vector.tensor_tensor(out=shift[:], in0=scaled[:], in1=betak_c, op=ADD)
 
         project_kf(0)
         for band in range(1, BANDS):

@@ -22,16 +22,14 @@ GROUPS = 2
 HEIGHT = 24
 WIDTH = 48
 POSITIONS = HEIGHT * WIDTH
-BAND_ROWS = 8
-BANDS = HEIGHT // BAND_ROWS
-BAND = BAND_ROWS * WIDTH
-SLICE = 128
-SLICES = BAND // SLICE
-BLOCKS = POSITIONS // SLICE
+PAIRS = POSITIONS // 2
 HALVES = 2
 LEVELS = (1, 3, 6, 8)
 TOKENS = 110
 EPS = 1e-5
+CHUNKS = ((0, 256), (256, 256), (512, 256), (768, 256), (1024, 128))
+LAST = len(CHUNKS) - 1
+LOADS = ((0, 256), (256, 512), (768, 384))
 
 FLOPS = 2 * 512 * 1024 * POSITIONS
 
@@ -49,109 +47,137 @@ def tile_apnb_pa_kernel(
         x_rows = feats[0].rearrange("(g p t) h w -> g p t (h w)", p=P, t=PACK)
         kf_out = out_0[0].rearrange("(m p) h w -> p m (h w)", p=P)
         raw = {}
+        grouped = {}
         codes = {}
         scales = {}
+        kf_acc = {}
+        val_acc = {}
         kf = {}
-        val = {}
 
-        def load_band(band):
-            for g in range(GROUPS):
-                raw[g, band] = keep.tile([P, PACK, BAND], BF16, name="raw_%d_%d" % (g, band))
-                nc.sync.dma_start(out=raw[g, band][:], in_=x_rows[g, :, :, band * BAND : (band + 1) * BAND])
+        def load(which_load, g):
+            first, width = LOADS[which_load]
+            raw[g, which_load] = keep.tile([P, PACK, width], BF16, name="raw_%d_%d" % (g, which_load))
+            nc.sync.dma_start(out=raw[g, which_load][:], in_=x_rows[g, :, :, first : first + width])
 
-        def regroup_and_quantise(band):
-            grouped = keep.tile([P, GROUPS, BAND, PACK], BF16, name="grouped_%d" % band, align_bytes=64)
-            for g in range(GROUPS):
-                nc.vector.tensor_copy(
-                    out=grouped[:, g].rearrange("p (c i) t -> p c t i", i=4),
-                    in_=raw[g, band][:].rearrange("p t (c i) -> p c t i", i=4),
+        def load_weight(wt, words, scales_in):
+            for quad in range(4):
+                nc.sync.dma_start(
+                    out=w_planes[32 * quad : 32 * quad + 4, wt].bitcast(I32),
+                    in_=scales_in.bitcast(I32)[:, 4 * quad : 4 * quad + 4, :].rearrange("g r n -> r g n"),
                 )
-            codes[band] = keep.tile([P, GROUPS * BAND], U32, name="codes_%d" % band, align_bytes=64)
-            scales[band] = keep.tile([P, GROUPS * BAND], U8, name="scales_%d" % band, align_bytes=64)
-            flat = grouped[:].rearrange("p g c t -> p (g c t)")
-            for first, width in ((0, 512), (512, 256)):
-                nc.vector.quantize_mx(
-                    out=codes[band][:, first : first + width].bitcast(FP8X4),
-                    scales=scales[band][:, first : first + width],
-                    in_=flat[:, PACK * first : PACK * (first + width)],
+            nc.sync.dma_start(out=w_words[:, wt].bitcast(I32), in_=words.bitcast(I32).rearrange("g p n -> p g n"))
+
+        def regroup(j, g, engine_copy):
+            first, width = CHUNKS[j]
+            if g == 0:
+                grouped[j] = keep.tile([P, GROUPS, width, PACK], BF16, name="grouped_%d" % j, align_bytes=64)
+            which_load = [n for n, (lo, w) in enumerate(LOADS) if lo <= first and first + width <= lo + w][0]
+            off = first - LOADS[which_load][0]
+            src = raw[g, which_load][:, :, off : off + width]
+            if j < LAST:
+                engine_copy(
+                    out=grouped[j][:, g].rearrange("p (par c i) t -> p par c t i", par=2, i=4),
+                    in_=src.rearrange("p t (c i par) -> p par c t i", par=2, i=4),
+                )
+            else:
+                engine_copy(
+                    out=grouped[j][:, g].rearrange("p (c i) t -> p c t i", i=4),
+                    in_=src.rearrange("p t (c i) -> p c t i", i=4),
                 )
 
-        def project_kf(band):
-            kf[band] = keep.tile([P, HALVES, BAND], F32, name="kf_%d" % band)
+        def quantise(j):
+            width = CHUNKS[j][1]
+            codes[j] = keep.tile([P, GROUPS * width], U32, name="codes_%d" % j, align_bytes=64)
+            scales[j] = keep.tile([P, GROUPS * width], U8, name="scales_%d" % j, align_bytes=64)
+            nc.vector.quantize_mx(
+                out=codes[j][:].bitcast(FP8X4),
+                scales=scales[j][:],
+                in_=grouped[j][:].rearrange("p g c t -> p (g c t)"),
+            )
+
+        def project_val(j):
+            width = CHUNKS[j][1]
+            slices = [(g, s) for s in range(width // P) for g in range(GROUPS)]
             for m in range(HALVES):
-                acc = psum.tile([P, BAND], F32, tag="kf", bufs=4)
-                for s in range(SLICES):
+                for n, (g, s) in enumerate(slices):
+                    cols = slice(g * width + s * P, g * width + (s + 1) * P)
+                    nc.tensor.matmul_mx(
+                        out=val_acc[j][:, m * P : (m + 1) * P],
+                        lhsT=codes[j][:, cols].bitcast(FP8X4),
+                        lhsT_scale=scales[j][:, cols],
+                        rhs=w_words[:, 1, g, 2 * P * m : 2 * P * (m + 1)].bitcast(FP4X4),
+                        rhs_scale=w_planes[:, 1, g, P * m : P * (m + 1)],
+                        start=(n == 0),
+                        stop=(n == len(slices) - 1),
+                    )
+
+        def project_kf(j):
+            width = CHUNKS[j][1]
+            for m in range(HALVES):
+                for s in range(width // P):
                     for g in range(GROUPS):
-                        cols = slice(g * BAND + s * SLICE, g * BAND + (s + 1) * SLICE)
+                        cols = slice(g * width + s * P, g * width + (s + 1) * P)
                         nc.tensor.matmul_mx(
-                            out=acc[:, s * SLICE : (s + 1) * SLICE],
+                            out=kf_acc[j][:, m, s * P : (s + 1) * P],
                             lhsT=w_words[:, 0, g, 2 * P * m : 2 * P * (m + 1)].bitcast(FP4X4),
                             lhsT_scale=w_planes[:, 0, g, P * m : P * (m + 1)],
-                            rhs=codes[band][:, cols].bitcast(FP8X4),
-                            rhs_scale=scales[band][:, cols],
+                            rhs=codes[j][:, cols].bitcast(FP8X4),
+                            rhs_scale=scales[j][:, cols],
                             start=(g == 0),
                             stop=(g == GROUPS - 1),
                         )
+
+        def norm_relu(j):
+            first, width = CHUNKS[j]
+            kf[j] = keep.tile([P, HALVES, width], F32, name="kf_%d" % j)
+            for m in range(HALVES):
+                if j < LAST:
+                    out = kf[j][:, m, :].rearrange("p (u par) -> p u par", par=2)
+                    in_ = kf_acc[j][:, m, :].rearrange("p (par u) -> p u par", par=2)
+                else:
+                    out = kf[j][:, m, :]
+                    in_ = kf_acc[j][:, m, :]
                 nc.scalar.activation(
-                    out=kf[band][:, m, :], in_=acc[:], func=ACT.Relu, bias=shift[:, m : m + 1], scale=gain[:, m : m + 1]
+                    out=out, in_=in_, func=ACT.Relu, bias=shift[:, m : m + 1], scale=gain[:, m : m + 1]
                 )
-            nc.sync.dma_start(out=kf_out[:, :, band * BAND : (band + 1) * BAND], in_=kf[band][:])
+            nc.sync.dma_start(out=kf_out[:, :, first : first + width], in_=kf[j][:])
 
-        def project_val(band):
-            for s in range(SLICES):
-                val_acc = psum.tile([P, HALVES * P], F32, tag="val", bufs=3)
-                for m in range(HALVES):
-                    for g in range(GROUPS):
-                        cols = slice(g * BAND + s * SLICE, g * BAND + (s + 1) * SLICE)
-                        nc.tensor.matmul_mx(
-                            out=val_acc[:, m * P : (m + 1) * P],
-                            lhsT=codes[band][:, cols].bitcast(FP8X4),
-                            lhsT_scale=scales[band][:, cols],
-                            rhs=w_words[:, 1, g, 2 * P * m : 2 * P * (m + 1)].bitcast(FP4X4),
-                            rhs_scale=w_planes[:, 1, g, P * m : P * (m + 1)],
-                            start=(g == 0),
-                            stop=(g == GROUPS - 1),
-                        )
-                block = band * SLICES + s
-                val[block] = keep.tile([P, HALVES * P], F32, name="val_%d" % block)
-                nc.scalar.copy(out=val[block][:], in_=val_acc[:])
+        def pool_val(j, stop):
+            nc.tensor.matmul(out=value_acc[:], lhsT=pool_mat[:, j, :], rhs=val[:, j, :], start=False, stop=stop)
 
-        def pool_val(band):
-            for block in range(band * SLICES, (band + 1) * SLICES):
-                nc.tensor.matmul(
-                    out=value_acc[:], lhsT=pool_mat[:, block, :], rhs=val[block][:], start=(block == 0), stop=False
-                )
-
-        def pool_kf(band):
-            halves = kf[band][:].rearrange("p q (n two) -> p q n two", two=2)
-            pair = keep.tile([P, HALVES, BAND // 2], F32, name="pair_%d" % band)
-            nc.vector.tensor_tensor(out=pair[:], in0=halves[:, :, :, 0], in1=halves[:, :, :, 1], op=ADD)
-            nc.vector.tensor_reduce(
-                out=row_sums8[:, :, 64 * band : 64 * (band + 1)],
-                in_=pair[:].rearrange("p q (n j) -> p q n j", j=3),
-                axis=AXIS.X,
-                op=ADD,
+        def add_pairs(j):
+            first, width = CHUNKS[j]
+            halves = kf[j][:].rearrange("p q (n two) -> p q n two", two=2)
+            nc.vector.tensor_tensor(
+                out=pair[:, :, first // 2 : (first + width) // 2], in0=halves[:, :, :, 0], in1=halves[:, :, :, 1], op=ADD
             )
-            for a in (2 * band, 2 * band + 1):
-                rows = pair[:, :, 96 * (a - 2 * band) : 96 * (a - 2 * band + 1)]
+
+        def pool_cells(s, a0, a1):
+            rows, wide = HEIGHT // s, WIDTH // 2 // s
+            per = rows * (WIDTH // 2)
+            t0 = first_token[s]
+            if a1 - a0 == 1:
                 nc.vector.tensor_reduce(
-                    out=tok[:, :, first_token[6] + 6 * a : first_token[6] + 6 * (a + 1)],
-                    in_=rows.rearrange("p q (i b j) -> p q b i j", i=4, b=6, j=4),
+                    out=tok[:, :, t0 + s * a0 : t0 + s * a1],
+                    in_=pair[:, :, per * a0 : per * a1].rearrange("p q (i b j) -> p q b i j", i=rows, b=s, j=wide),
                     axis=AXIS.XY,
                     op=ADD,
                 )
-            a_done, a_new = (BAND_ROWS * band) // 3, (BAND_ROWS * (band + 1)) // 3
+            else:
+                for q in range(HALVES):
+                    nc.vector.tensor_reduce(
+                        out=tok[:, q, t0 + s * a0 : t0 + s * a1].rearrange("p (a b) -> p a b", b=s),
+                        in_=pair[:, q, per * a0 : per * a1].rearrange(
+                            "p (a i b j) -> p a b i j", i=rows, b=s, j=wide
+                        ),
+                        axis=AXIS.XY,
+                        op=ADD,
+                    )
+
+        def pool_level3(a):
             nc.vector.tensor_reduce(
-                out=tok[:, :, first_token[8] + 8 * a_done : first_token[8] + 8 * a_new].rearrange(
-                    "p q (a b) -> p q a b", b=8
-                ),
-                in_=row_sums8[:, :, 24 * a_done : 24 * a_new].rearrange("p q (a i b) -> p q a b i", i=3, b=8),
-                axis=AXIS.X,
-                op=ADD,
-            )
-            nc.vector.tensor_reduce(
-                out=tok[:, :, first_token[3] + 3 * band : first_token[3] + 3 * (band + 1)],
-                in_=tok[:, :, first_token[6] + 12 * band : first_token[6] + 12 * (band + 1)].rearrange(
+                out=tok[:, :, first_token[3] + 3 * a : first_token[3] + 3 * (a + 1)],
+                in_=tok[:, :, first_token[6] + 12 * a : first_token[6] + 12 * (a + 1)].rearrange(
                     "p q (a b j) -> p q b a j", a=2, b=3, j=2
                 ),
                 axis=AXIS.XY,
@@ -167,19 +193,15 @@ def tile_apnb_pa_kernel(
         nc.vector.memset(bv_row[:], 0.0)
         one = keep.tile([P, 1], F32)
         nc.vector.memset(one[:], 1.0)
-        pool_mat = keep.tile([P, BLOCKS, P], F32)
-        nc.vector.memset(pool_mat[:], 0.0)
 
-        load_band(0)
-        for wt, words, scales_in in ((1, Wv_words, Wv_scales), (0, Wk_words, Wk_scales)):
-            for quad in range(4):
-                nc.sync.dma_start(
-                    out=w_planes[32 * quad : 32 * quad + 4, wt].bitcast(I32),
-                    in_=scales_in.bitcast(I32)[:, 4 * quad : 4 * quad + 4, :].rearrange("g r n -> r g n"),
-                )
-            nc.sync.dma_start(out=w_words[:, wt].bitcast(I32), in_=words.bitcast(I32).rearrange("g p n -> p g n"))
-        load_band(1)
-        load_band(2)
+        load(0, 0)
+        load(0, 1)
+        load_weight(1, Wv_words, Wv_scales)
+        load(1, 0)
+        load(1, 1)
+        load_weight(0, Wk_words, Wk_scales)
+        load(2, 0)
+        load(2, 1)
         for v, vec in enumerate((bk, gk, betak, mk, vk)):
             nc.scalar.dma_start(out=vec_rows[2 * v : 2 * v + 2, :], in_=vec.rearrange("(m c) -> m c", m=2))
         nc.scalar.dma_start(out=bv_row[0:1, :], in_=bv.rearrange("(o c) -> o c", o=1))
@@ -188,13 +210,27 @@ def tile_apnb_pa_kernel(
         make_identity(nc, ident[:])
         warm = keep.tile([P, 1], F32)
         nc.scalar.activation(out=warm[:], in_=one[:], func=ACT.Abs_reciprocal_sqrt)
+        pool_mat = keep.tile([P, len(CHUNKS), P], F32)
+        nc.gpsimd.memset(pool_mat[:], 0.0)
+        nines_bf = keep.tile([P, P], BF16)
+        nc.gpsimd.memset(nines_bf[:], 9.0)
+        ones = keep.tile([P, TOKENS], F32)
+        nc.gpsimd.memset(ones[:], 1.0)
+        inv_size = keep.tile([P, TOKENS], F32)
+        for s in LEVELS:
+            cells = slice(first_token[s], first_token[s] + s * s)
+            nc.gpsimd.tensor_scalar_mul(out=inv_size[:, cells], in0=ones[:, cells], scalar1=float(s * s) / POSITIONS)
 
-        where = keep.tile([P, POSITIONS], BF16)
+        where = keep.tile([P, PAIRS + P], BF16)
         nc.vector.tensor_tensor(
-            out=where[:].rearrange("p (h c two) -> p h c two", h=HEIGHT, two=2),
-            in0=ident[:, 0:HEIGHT].unsqueeze(2).unsqueeze(3).to_broadcast([P, HEIGHT, WIDTH // 2, 2]),
-            in1=ident[:, HEIGHT : 2 * HEIGHT].unsqueeze(1).unsqueeze(3).to_broadcast([P, HEIGHT, WIDTH // 2, 2]),
+            out=where[:, 0:PAIRS].rearrange("p (h c) -> p h c", h=HEIGHT),
+            in0=ident[:, 0:HEIGHT].unsqueeze(2).to_broadcast([P, HEIGHT, WIDTH // 2]),
+            in1=ident[:, HEIGHT : 2 * HEIGHT].unsqueeze(1).to_broadcast([P, HEIGHT, WIDTH // 2]),
             op=ADD,
+        )
+        nc.vector.tensor_copy(
+            out=where[:, PAIRS : PAIRS + P].rearrange("p (n two) -> p n two", two=2),
+            in_=where[:, PAIRS - P // 2 : PAIRS].unsqueeze(2).to_broadcast([P, P // 2, 2]),
         )
         which = keep.tile([P, TOKENS], BF16)
         for s in LEVELS:
@@ -213,51 +249,58 @@ def tile_apnb_pa_kernel(
                 op0=MULT,
                 op1=ADD,
             )
-        hits = {}
-        for first in range(0, BLOCKS, 4):
-            hits[first] = psum.tile([P, 4, TOKENS], F32, tag="val", bufs=3, name="hits_%d" % first)
-            for j in range(min(4, BLOCKS - first)):
-                nc.tensor.matmul(
-                    out=hits[first][:, j, :],
-                    lhsT=where[:, (first + j) * P : (first + j + 1) * P],
-                    rhs=which[:],
-                    start=True,
-                    stop=True,
-                )
-        nines_bf = keep.tile([P, P], BF16)
-        nc.vector.memset(nines_bf[:], 9.0)
+        hits_a = psum.tile([P, LAST, TOKENS], F32, tag="value")
+        hits_b = psum.tile([P, 1, TOKENS], F32, tag="kf_3")
+        for j in range(len(CHUNKS)):
+            first = j * P if j < LAST else PAIRS
+            nc.tensor.matmul(
+                out=hits_a[:, j, :] if j < LAST else hits_b[:, 0, :],
+                lhsT=where[:, first : first + P],
+                rhs=which[:],
+                start=True,
+                stop=True,
+            )
         ident_bf = keep.tile([P, P], BF16)
         nc.vector.tensor_copy(out=ident_bf[:], in_=ident[:])
-        row_sums8 = keep.tile([P, HALVES, HEIGHT * 8], F32)
+        pair = keep.tile([P, HALVES, PAIRS], F32)
         tok = keep.tile([P, HALVES, TOKENS], F32)
+        val = keep.tile([P, len(CHUNKS), HALVES * P], F32)
 
-        regroup_and_quantise(0)
-
-        for first in range(0, BLOCKS, 4):
-            count = min(4, BLOCKS - first)
-            nc.scalar.activation(
-                out=pool_mat[:, first : first + count, 0:TOKENS], in_=hits[first][:, 0:count, :], func=ACT.Relu, bias=-1.0
-            )
-
-        ones = keep.tile([P, TOKENS], F32)
-        nc.gpsimd.memset(ones[:], 1.0)
-        inv_size = keep.tile([P, TOKENS], F32)
-        for s in LEVELS:
-            cells = slice(first_token[s], first_token[s] + s * s)
-            nc.gpsimd.tensor_scalar_mul(out=inv_size[:, cells], in0=ones[:, cells], scalar1=float(s * s) / POSITIONS)
-
-        value_acc = psum.tile([P, HALVES * P], F32, tag="value")
-        regroup_and_quantise(1)
-
+        regroup(0, 0, nc.vector.tensor_copy)
+        regroup(0, 1, nc.scalar.copy)
+        regroup(1, 0, nc.vector.tensor_copy)
+        regroup(1, 1, nc.scalar.copy)
+        quantise(0)
+        val_01 = psum.tile([P, 2, HALVES * P], F32, tag="val_01")
+        val_acc[0], val_acc[1] = val_01[:, 0, :], val_01[:, 1, :]
         project_val(0)
-
-        vec_t = psum.tile([P, P], BF16, tag="kf", bufs=4)
+        vec_t = psum.tile([P, P], BF16, tag="last")
         nc.tensor.transpose(vec_t[:], vec_rows[:], ident_bf[:])
+        kf_acc[0] = psum.tile([P, HALVES, 2 * P], F32, tag="kf_0", name="kf_acc_0")
+        project_kf(0)
+
+        regroup(2, 0, nc.vector.tensor_copy)
+        regroup(2, 1, nc.scalar.copy)
+        quantise(1)
+        project_val(1)
+        kf_acc[1] = psum.tile([P, HALVES, 2 * P], F32, tag="kf_1", name="kf_acc_1")
+        project_kf(1)
+
         per_ch = keep.tile([P, 10], F32)
         nc.scalar.copy(out=per_ch[:], in_=vec_t[:, 0:10])
         bk_c, gk_c, betak_c, mk_c, vk_c = [per_ch[:, 2 * v : 2 * v + 2] for v in range(5)]
         inv_std = keep.tile([P, 2], F32)
         nc.scalar.activation(out=inv_std[:], in_=vk_c, func=ACT.Abs_reciprocal_sqrt, bias=EPS)
+
+        regroup(3, 0, nc.vector.tensor_copy)
+        regroup(3, 1, nc.scalar.copy)
+        quantise(2)
+        val_23 = psum.tile([P, 2, HALVES * P], F32, tag="val_23")
+        val_acc[2], val_acc[3] = val_23[:, 0, :], val_23[:, 1, :]
+        project_val(2)
+        kf_acc[2] = psum.tile([P, HALVES, 2 * P], F32, tag="kf_2", name="kf_acc_2")
+        project_kf(2)
+
         centred = keep.tile([P, 2], F32)
         nc.vector.tensor_tensor(out=centred[:], in0=bk_c, in1=mk_c, op=SUBTRACT)
         gain = keep.tile([P, 2], F32)
@@ -267,17 +310,51 @@ def tile_apnb_pa_kernel(
         shift = keep.tile([P, 2], F32)
         nc.vector.tensor_tensor(out=shift[:], in0=scaled[:], in1=betak_c, op=ADD)
 
-        project_kf(0)
-        for band in range(1, BANDS):
-            if band + 1 < BANDS:
-                regroup_and_quantise(band + 1)
-            project_val(band)
-            project_kf(band)
-            pool_val(band - 1)
-            pool_kf(band - 1)
-        pool_val(BANDS - 1)
-        nc.tensor.matmul(out=value_acc[:], lhsT=nines_bf[:], rhs=bv_row[:], start=False, stop=True)
-        pool_kf(BANDS - 1)
+        regroup(4, 0, nc.vector.tensor_copy)
+        nc.scalar.activation(out=pool_mat[:, LAST, 0:TOKENS], in_=hits_b[:, 0, :], func=ACT.Relu, bias=-1.0)
+        norm_relu(0)
+        regroup(4, 1, nc.scalar.copy)
+        quantise(3)
+        project_val(3)
+        kf_acc[3] = psum.tile([P, HALVES, 2 * P], F32, tag="kf_3", name="kf_acc_3")
+        project_kf(3)
+        add_pairs(0)
+        quantise(4)
+        last = psum.tile([P, 4, P], F32, tag="last")
+        kf_acc[4], val_acc[4] = last[:, 0:2, :], last[:, 2:4, :].rearrange("p a b -> p (a b)")
+        project_kf(4)
+        project_val(4)
+
+        norm_relu(1)
+        add_pairs(1)
+        pool_cells(8, 0, 3)
+        norm_relu(2)
+        pool_cells(6, 0, 2)
+        pool_level3(0)
+        add_pairs(2)
+        norm_relu(3)
+        add_pairs(3)
+        norm_relu(4)
+        pool_cells(8, 3, 7)
+        pool_cells(6, 2, 5)
+        pool_level3(1)
+
+        nc.scalar.activation(out=pool_mat[:, 0:LAST, 0:TOKENS], in_=hits_a[:], func=ACT.Relu, bias=-1.0)
+        nc.scalar.copy(out=val[:, 0:2, :], in_=val_01[:])
+        value_acc = psum.tile([P, HALVES * P], F32, tag="value")
+        nc.tensor.matmul(out=value_acc[:], lhsT=nines_bf[:], rhs=bv_row[:], start=True, stop=False)
+        pool_val(0, False)
+        pool_val(1, False)
+        nc.scalar.copy(out=val[:, 2:4, :], in_=val_23[:])
+        pool_val(2, False)
+        pool_val(3, False)
+        nc.scalar.copy(out=val[:, 4, :], in_=val_acc[4])
+        pool_val(4, True)
+
+        add_pairs(4)
+        pool_cells(8, 7, 8)
+        pool_cells(6, 5, 6)
+        pool_level3(2)
 
         value_sb = keep.tile([P, HALVES * P], F32)
         nc.scalar.mul(out=value_sb[:], in_=value_acc[:], mul=1.0 / 9.0)

@@ -59,13 +59,15 @@ def tile_apnb_pa_kernel(
             raw[g, which_load] = keep.tile([P, PACK, width], BF16, name="raw_%d_%d" % (g, which_load))
             nc.sync.dma_start(out=raw[g, which_load][:], in_=x_rows[g, :, :, first : first + width])
 
-        def load_weight(wt, words, scales_in):
+        def load_words(wt, words):
+            nc.sync.dma_start(out=w_words[:, wt].bitcast(I32), in_=words.bitcast(I32).rearrange("g p n -> p g n"))
+
+        def load_scales(wt, scales_in):
             for quad in range(4):
                 nc.sync.dma_start(
                     out=w_planes[32 * quad : 32 * quad + 4, wt].bitcast(I32),
                     in_=scales_in.bitcast(I32)[:, 4 * quad : 4 * quad + 4, :].rearrange("g r n -> r g n"),
                 )
-            nc.sync.dma_start(out=w_words[:, wt].bitcast(I32), in_=words.bitcast(I32).rearrange("g p n -> p g n"))
 
         def regroup(j, g, engine_copy):
             first, width = CHUNKS[j]
@@ -155,10 +157,9 @@ def tile_apnb_pa_kernel(
         def pool_cells(s, a0, a1):
             rows, wide = HEIGHT // s, WIDTH // 2 // s
             per = rows * (WIDTH // 2)
-            t0 = first_token[s]
             if a1 - a0 == 1:
                 nc.vector.tensor_reduce(
-                    out=tok[:, :, t0 + s * a0 : t0 + s * a1],
+                    out=tok[s][:, :, s * a0 : s * a1],
                     in_=pair[:, :, per * a0 : per * a1].rearrange("p q (i b j) -> p q b i j", i=rows, b=s, j=wide),
                     axis=AXIS.XY,
                     op=ADD,
@@ -166,7 +167,7 @@ def tile_apnb_pa_kernel(
             else:
                 for q in range(HALVES):
                     nc.vector.tensor_reduce(
-                        out=tok[:, q, t0 + s * a0 : t0 + s * a1].rearrange("p (a b) -> p a b", b=s),
+                        out=tok[s][:, q, s * a0 : s * a1].rearrange("p (a b) -> p a b", b=s),
                         in_=pair[:, q, per * a0 : per * a1].rearrange(
                             "p (a i b j) -> p a b i j", i=rows, b=s, j=wide
                         ),
@@ -176,8 +177,8 @@ def tile_apnb_pa_kernel(
 
         def pool_level3(a):
             nc.vector.tensor_reduce(
-                out=tok[:, :, first_token[3] + 3 * a : first_token[3] + 3 * (a + 1)],
-                in_=tok[:, :, first_token[6] + 12 * a : first_token[6] + 12 * (a + 1)].rearrange(
+                out=tok[3][:, :, 3 * a : 3 * (a + 1)],
+                in_=tok[6][:, :, 12 * a : 12 * (a + 1)].rearrange(
                     "p q (a b j) -> p q b a j", a=2, b=3, j=2
                 ),
                 axis=AXIS.XY,
@@ -187,39 +188,38 @@ def tile_apnb_pa_kernel(
         w_words = keep.tile([P, 2, GROUPS, 4 * P], U8, align_bytes=64)
         w_planes = keep.tile([P, 2, GROUPS, 2 * P], U8, align_bytes=64)
         nc.vector.memset(w_planes[:].bitcast(I32), 0)
-        vec_rows = keep.tile([P, P], BF16)
-        nc.vector.memset(vec_rows[:], 0.0)
-        bv_row = keep.tile([P, HALVES * P], BF16)
-        nc.vector.memset(bv_row[:], 0.0)
-        one = keep.tile([P, 1], F32)
-        nc.vector.memset(one[:], 1.0)
-
-        load(0, 0)
-        load(0, 1)
-        load_weight(1, Wv_words, Wv_scales)
-        load(1, 0)
-        load(1, 1)
-        load_weight(0, Wk_words, Wk_scales)
-        load(2, 0)
-        load(2, 1)
-        for v, vec in enumerate((bk, gk, betak, mk, vk)):
-            nc.scalar.dma_start(out=vec_rows[2 * v : 2 * v + 2, :], in_=vec.rearrange("(m c) -> m c", m=2))
-        nc.scalar.dma_start(out=bv_row[0:1, :], in_=bv.rearrange("(o c) -> o c", o=1))
-
         ident = keep.tile([P, P], F32)
         make_identity(nc, ident[:])
+        vec_rows = keep.tile([P, P], BF16)
+        nc.gpsimd.memset(vec_rows[:], 0.0)
+        bv_row = keep.tile([P, HALVES * P], BF16)
+        nc.gpsimd.memset(bv_row[:], 0.0)
+
+        def load_vector(queue, v, vec):
+            queue.dma_start(out=vec_rows[2 * v : 2 * v + 2, :], in_=vec.rearrange("(m c) -> m c", m=2))
+
+        load(0, 1)
+        load(0, 0)
+        load(1, 1)
+        load(1, 0)
+        load_scales(1, Wv_scales)
+        load_words(1, Wv_words)
+        load(2, 1)
+        load(2, 0)
+        load_words(0, Wk_words)
+        load_vector(nc.sync, 0, bk)
+        load_vector(nc.sync, 3, mk)
+        load_scales(0, Wk_scales)
+        nc.sync.dma_start(out=bv_row[0:1, :], in_=bv.rearrange("(o c) -> o c", o=1))
+        load_vector(nc.gpsimd, 4, vk)
+        load_vector(nc.gpsimd, 1, gk)
+        load_vector(nc.gpsimd, 2, betak)
+
         warm = keep.tile([P, 1], F32)
-        nc.scalar.activation(out=warm[:], in_=one[:], func=ACT.Abs_reciprocal_sqrt)
+        nc.scalar.activation(out=warm[:], in_=ident[:, 0:1], func=ACT.Abs_reciprocal_sqrt, bias=1.0)
         pool_mat = keep.tile([P, len(CHUNKS), P], F32)
-        nc.gpsimd.memset(pool_mat[:], 0.0)
         nines_bf = keep.tile([P, P], BF16)
         nc.gpsimd.memset(nines_bf[:], 9.0)
-        ones = keep.tile([P, TOKENS], F32)
-        nc.gpsimd.memset(ones[:], 1.0)
-        inv_size = keep.tile([P, TOKENS], F32)
-        for s in LEVELS:
-            cells = slice(first_token[s], first_token[s] + s * s)
-            nc.gpsimd.tensor_scalar_mul(out=inv_size[:, cells], in0=ones[:, cells], scalar1=float(s * s) / POSITIONS)
 
         where = keep.tile([P, PAIRS + P], BF16)
         nc.vector.tensor_tensor(
@@ -262,45 +262,45 @@ def tile_apnb_pa_kernel(
             )
         ident_bf = keep.tile([P, P], BF16)
         nc.vector.tensor_copy(out=ident_bf[:], in_=ident[:])
+        nc.vector.memset(pool_mat[:, :, TOKENS:P], 0.0)
         pair = keep.tile([P, HALVES, PAIRS], F32)
-        tok = keep.tile([P, HALVES, TOKENS], F32)
+        tok = {}
+        for s in LEVELS:
+            tok[s] = keep.tile([P, HALVES, s * s], F32, name="tok_%d" % s)
         val = keep.tile([P, len(CHUNKS), HALVES * P], F32)
+
+        val_01 = psum.tile([P, 2, HALVES * P], F32, tag="val_01")
+        val_acc[0], val_acc[1] = val_01[:, 0, :], val_01[:, 1, :]
+        val_23 = psum.tile([P, 2, HALVES * P], F32, tag="val_23")
+        val_acc[2], val_acc[3] = val_23[:, 0, :], val_23[:, 1, :]
+        kf_acc[0] = psum.tile([P, HALVES, 2 * P], F32, tag="kf_0", name="kf_acc_0")
+        kf_acc[1] = psum.tile([P, HALVES, 2 * P], F32, tag="kf_1", name="kf_acc_1")
+        kf_acc[2] = psum.tile([P, HALVES, 2 * P], F32, tag="kf_2", name="kf_acc_2")
 
         regroup(0, 0, nc.vector.tensor_copy)
         regroup(0, 1, nc.scalar.copy)
+        quantise(0)
+        project_val(0)
         regroup(1, 0, nc.vector.tensor_copy)
         regroup(1, 1, nc.scalar.copy)
-        quantise(0)
-        val_01 = psum.tile([P, 2, HALVES * P], F32, tag="val_01")
-        val_acc[0], val_acc[1] = val_01[:, 0, :], val_01[:, 1, :]
-        project_val(0)
-        vec_t = psum.tile([P, P], BF16, tag="last")
-        nc.tensor.transpose(vec_t[:], vec_rows[:], ident_bf[:])
-        kf_acc[0] = psum.tile([P, HALVES, 2 * P], F32, tag="kf_0", name="kf_acc_0")
-        project_kf(0)
-
         regroup(2, 0, nc.vector.tensor_copy)
         regroup(2, 1, nc.scalar.copy)
         quantise(1)
         project_val(1)
-        kf_acc[1] = psum.tile([P, HALVES, 2 * P], F32, tag="kf_1", name="kf_acc_1")
+        vec_t = psum.tile([P, P], BF16, tag="last")
+        nc.tensor.transpose(vec_t[:], vec_rows[:], ident_bf[:])
+        project_kf(0)
         project_kf(1)
-
+        regroup(3, 0, nc.vector.tensor_copy)
+        regroup(3, 1, nc.scalar.copy)
         per_ch = keep.tile([P, 10], F32)
         nc.scalar.copy(out=per_ch[:], in_=vec_t[:, 0:10])
         bk_c, gk_c, betak_c, mk_c, vk_c = [per_ch[:, 2 * v : 2 * v + 2] for v in range(5)]
         inv_std = keep.tile([P, 2], F32)
         nc.scalar.activation(out=inv_std[:], in_=vk_c, func=ACT.Abs_reciprocal_sqrt, bias=EPS)
-
-        regroup(3, 0, nc.vector.tensor_copy)
-        regroup(3, 1, nc.scalar.copy)
         quantise(2)
-        val_23 = psum.tile([P, 2, HALVES * P], F32, tag="val_23")
-        val_acc[2], val_acc[3] = val_23[:, 0, :], val_23[:, 1, :]
         project_val(2)
-        kf_acc[2] = psum.tile([P, HALVES, 2 * P], F32, tag="kf_2", name="kf_acc_2")
         project_kf(2)
-
         centred = keep.tile([P, 2], F32)
         nc.vector.tensor_tensor(out=centred[:], in0=bk_c, in1=mk_c, op=SUBTRACT)
         gain = keep.tile([P, 2], F32)
@@ -309,59 +309,62 @@ def tile_apnb_pa_kernel(
         nc.vector.tensor_tensor(out=scaled[:], in0=centred[:], in1=gain[:], op=MULT)
         shift = keep.tile([P, 2], F32)
         nc.vector.tensor_tensor(out=shift[:], in0=scaled[:], in1=betak_c, op=ADD)
-
         regroup(4, 0, nc.vector.tensor_copy)
-        nc.scalar.activation(out=pool_mat[:, LAST, 0:TOKENS], in_=hits_b[:, 0, :], func=ACT.Relu, bias=-1.0)
-        norm_relu(0)
         regroup(4, 1, nc.scalar.copy)
+        nc.scalar.activation(out=pool_mat[:, LAST, 0:TOKENS], in_=hits_b[:, 0, :], func=ACT.Relu, bias=-1.0)
         quantise(3)
         project_val(3)
         kf_acc[3] = psum.tile([P, HALVES, 2 * P], F32, tag="kf_3", name="kf_acc_3")
         project_kf(3)
-        add_pairs(0)
         quantise(4)
         last = psum.tile([P, 4, P], F32, tag="last")
         kf_acc[4], val_acc[4] = last[:, 0:2, :], last[:, 2:4, :].rearrange("p a b -> p (a b)")
         project_kf(4)
         project_val(4)
 
+        keyp = keep.tile([P, HALVES, TOKENS], F32)
+
+        def mean(s):
+            cells = slice(first_token[s], first_token[s] + s * s)
+            nc.scalar.mul(out=keyp[:, :, cells], in_=tok[s][:], mul=float(s * s) / POSITIONS)
+
+        norm_relu(0)
+        add_pairs(0)
         norm_relu(1)
         add_pairs(1)
         pool_cells(8, 0, 3)
-        norm_relu(2)
-        pool_cells(6, 0, 2)
-        pool_level3(0)
-        add_pairs(2)
-        norm_relu(3)
-        add_pairs(3)
-        norm_relu(4)
-        pool_cells(8, 3, 7)
-        pool_cells(6, 2, 5)
-        pool_level3(1)
-
         nc.scalar.activation(out=pool_mat[:, 0:LAST, 0:TOKENS], in_=hits_a[:], func=ACT.Relu, bias=-1.0)
         nc.scalar.copy(out=val[:, 0:2, :], in_=val_01[:])
         value_acc = psum.tile([P, HALVES * P], F32, tag="value")
         nc.tensor.matmul(out=value_acc[:], lhsT=nines_bf[:], rhs=bv_row[:], start=True, stop=False)
         pool_val(0, False)
         pool_val(1, False)
+        norm_relu(2)
+        pool_cells(6, 0, 2)
+        pool_level3(0)
+        add_pairs(2)
+        norm_relu(3)
+        add_pairs(3)
         nc.scalar.copy(out=val[:, 2:4, :], in_=val_23[:])
         pool_val(2, False)
         pool_val(3, False)
+        norm_relu(4)
+        pool_cells(8, 3, 7)
+        pool_cells(6, 2, 5)
+        pool_level3(1)
         nc.scalar.copy(out=val[:, 4, :], in_=val_acc[4])
         pool_val(4, True)
 
         add_pairs(4)
         pool_cells(8, 7, 8)
-        pool_cells(6, 5, 6)
-        pool_level3(2)
-
         value_sb = keep.tile([P, HALVES * P], F32)
         nc.scalar.mul(out=value_sb[:], in_=value_acc[:], mul=1.0 / 9.0)
         nc.sync.dma_start(out=out_2[0], in_=value_sb[0:TOKENS, :])
-        nc.vector.tensor_reduce(out=tok[:, :, 0], in_=tok[:, :, 1:10], axis=AXIS.X, op=ADD)
-        keyp = keep.tile([P, HALVES, TOKENS], F32)
-        nc.vector.tensor_tensor(
-            out=keyp[:], in0=tok[:], in1=inv_size[:].unsqueeze(1).to_broadcast([P, HALVES, TOKENS]), op=MULT
-        )
+        mean(8)
+        pool_cells(6, 5, 6)
+        mean(6)
+        pool_level3(2)
+        mean(3)
+        nc.vector.tensor_reduce(out=tok[1][:, :, 0], in_=tok[3][:], axis=AXIS.X, op=ADD)
+        mean(1)
         nc.sync.dma_start(out=out_1[0].rearrange("(m p) t -> p m t", p=P), in_=keyp[:])

@@ -27,6 +27,7 @@ HALVES = 2
 LEVELS = (1, 3, 6, 8)
 TOKENS = 110
 EPS = 1e-5
+LEAD = 6
 CHUNKS = ((0, 256), (256, 256), (512, 256), (768, 256), (1024, 128))
 LAST = len(CHUNKS) - 1
 LOADS = ((0, 256), (256, 512), (768, 384))
@@ -192,6 +193,9 @@ def tile_apnb_pa_kernel(
         make_identity(nc, ident[:])
         vec_rows = keep.tile([P, P], BF16)
         nc.gpsimd.memset(vec_rows[:], 0.0)
+        down = keep.tile([P, P], F32)
+        nc.gpsimd.memset(down[:, 0:1], 0.0)
+        nc.gpsimd.tensor_copy(out=down[:, 1:P], in_=ident[:, 0 : P - 1])
         bv_row = keep.tile([P, HALVES * P], BF16)
         nc.gpsimd.memset(bv_row[:], 0.0)
 
@@ -322,10 +326,10 @@ def tile_apnb_pa_kernel(
         project_kf(4)
         project_val(4)
 
-        keyp = keep.tile([P, HALVES, TOKENS], F32)
+        keyp = keep.tile([P, HALVES, LEAD + TOKENS], F32)
 
         def mean(s):
-            cells = slice(first_token[s], first_token[s] + s * s)
+            cells = slice(LEAD + first_token[s], LEAD + first_token[s] + s * s)
             nc.scalar.mul(out=keyp[:, :, cells], in_=tok[s][:], mul=float(s * s) / POSITIONS)
 
         norm_relu(0)
@@ -360,6 +364,10 @@ def tile_apnb_pa_kernel(
         value_sb = keep.tile([P, HALVES * P], F32)
         nc.scalar.mul(out=value_sb[:], in_=value_acc[:], mul=1.0 / 9.0)
         nc.sync.dma_start(out=out_2[0], in_=value_sb[0:TOKENS, :])
+        edge = keep.tile([P, HALVES, LEAD], F32)
+        nc.scalar.mul(out=edge[:], in_=tok[8][:, :, 64 - LEAD : 64], mul=64.0 / POSITIONS)
+        before = psum.tile([P, HALVES, LEAD], F32, tag="kf_0")
+        nc.tensor.matmul(out=before[:], lhsT=down[:], rhs=edge[:], start=True, stop=True)
         mean(8)
         pool_cells(6, 5, 6)
         mean(6)
@@ -367,4 +375,13 @@ def tile_apnb_pa_kernel(
         mean(3)
         nc.vector.tensor_reduce(out=tok[1][:, :, 0], in_=tok[3][:], axis=AXIS.X, op=ADD)
         mean(1)
-        nc.sync.dma_start(out=out_1[0].rearrange("(m p) t -> p m t", p=P), in_=keyp[:])
+        nc.scalar.copy(out=keyp[:, :, 0:LEAD], in_=before[:])
+        groups = out_1[0].rearrange("(m q j) t -> q m (j t)", m=HALVES, j=4)
+        for j in range(4):
+            borrowed, lent = (-2 * j) % 8, (-2 * (j + 1)) % 8
+            length = borrowed + TOKENS - lent
+            queue = nc.sync if j % 2 == 0 else nc.scalar
+            queue.dma_start(
+                out=groups[:, :, TOKENS * j - borrowed : TOKENS * j - borrowed + length],
+                in_=keyp[j:P:4, :, LEAD - borrowed : LEAD - borrowed + length],
+            )

@@ -30,7 +30,7 @@ EPS = 1e-5
 LEAD = 6
 CHUNKS = ((0, 256), (256, 256), (512, 256), (768, 256), (1024, 128))
 LAST = len(CHUNKS) - 1
-LOADS = ((0, 256), (256, 512), (768, 384))
+LOADS = ((0, 256), (256, 512), (768, 256), (1024, 128))
 
 FLOPS = 2 * 512 * 1024 * POSITIONS
 
@@ -214,6 +214,8 @@ def tile_apnb_pa_kernel(
         load_vector(nc.sync, 0, bk)
         load_vector(nc.sync, 3, mk)
         load_scales(0, Wk_scales)
+        load(3, 1)
+        load(3, 0)
         nc.sync.dma_start(out=bv_row[0:1, :], in_=bv.rearrange("(o c) -> o c", o=1))
         load_vector(nc.gpsimd, 4, vk)
         load_vector(nc.gpsimd, 1, gk)

@@ -365,7 +365,10 @@ def tile_apnb_pa_kernel(
         pool_cells(8, 7, 8)
         value_sb = keep.tile([P, HALVES * P], F32)
         nc.scalar.mul(out=value_sb[:], in_=value_acc[:], mul=1.0 / 9.0)
-        nc.sync.dma_start(out=out_2[0], in_=value_sb[0:TOKENS, :])
+        first_row = 0
+        for rows in (64, 32, 8, 4, 2):
+            nc.sync.dma_start(out=out_2[0, first_row : first_row + rows, :], in_=value_sb[first_row : first_row + rows, :])
+            first_row += rows
         edge = keep.tile([P, HALVES, LEAD], F32)
         nc.scalar.mul(out=edge[:], in_=tok[8][:, :, 64 - LEAD : 64], mul=64.0 / POSITIONS)
         before = psum.tile([P, HALVES, LEAD], F32, tag="kf_0")

@@ -13,6 +13,7 @@ FP4X4 = mybir.dt.float4_e2m1fn_x4
 ADD = mybir.AluOpType.add
 MULT = mybir.AluOpType.mult
 SUBTRACT = mybir.AluOpType.subtract
+MAX = mybir.AluOpType.max
 ACT = mybir.ActivationFunctionType
 AXIS = mybir.AxisListType
 
@@ -150,38 +151,35 @@ def tile_apnb_pa_kernel(
 
         def add_pairs(j):
             first, width = CHUNKS[j]
-            halves = kf[j][:].rearrange("p q (n two) -> p q n two", two=2)
+            halves = kf[j][:].rearrange("p q (n two) -> p n q two", two=2)
             nc.vector.tensor_tensor(
-                out=pair[:, :, first // 2 : (first + width) // 2], in0=halves[:, :, :, 0], in1=halves[:, :, :, 1], op=ADD
+                out=pair[:, first // 2 : (first + width) // 2, :], in0=halves[:, :, :, 0], in1=halves[:, :, :, 1], op=ADD
             )
 
-        def pool_cells(s, a0, a1):
+        def pool_row(s, a):
             rows, wide = HEIGHT // s, WIDTH // 2 // s
             per = rows * (WIDTH // 2)
-            if a1 - a0 == 1:
-                nc.vector.tensor_reduce(
-                    out=tok[s][:, :, s * a0 : s * a1],
-                    in_=pair[:, :, per * a0 : per * a1].rearrange("p q (i b j) -> p q b i j", i=rows, b=s, j=wide),
-                    axis=AXIS.XY,
-                    op=ADD,
-                )
-            else:
-                for q in range(HALVES):
-                    nc.vector.tensor_reduce(
-                        out=tok[s][:, q, s * a0 : s * a1].rearrange("p (a b) -> p a b", b=s),
-                        in_=pair[:, q, per * a0 : per * a1].rearrange(
-                            "p (a i b j) -> p a b i j", i=rows, b=s, j=wide
-                        ),
-                        axis=AXIS.XY,
-                        op=ADD,
-                    )
+            nc.vector.tensor_reduce(
+                out=tok[s][:, a, :, :],
+                in_=pair[:, per * a : per * (a + 1), :].rearrange("p (i b j) q -> p q b i j", i=rows, b=s, j=wide),
+                axis=AXIS.XY,
+                op=ADD,
+            )
+
+        def pool_rows(s, a0, a1, q):
+            rows, wide = HEIGHT // s, WIDTH // 2 // s
+            per = rows * (WIDTH // 2)
+            nc.vector.tensor_reduce(
+                out=tok[s][:, a0:a1, q, :],
+                in_=pair[:, per * a0 : per * a1, q].rearrange("p (a i b j) -> p a b i j", i=rows, b=s, j=wide),
+                axis=AXIS.XY,
+                op=ADD,
+            )
 
         def pool_level3(a):
             nc.vector.tensor_reduce(
-                out=tok[3][:, :, 3 * a : 3 * (a + 1)],
-                in_=tok[6][:, :, 12 * a : 12 * (a + 1)].rearrange(
-                    "p q (a b j) -> p q b a j", a=2, b=3, j=2
-                ),
+                out=tok[3][:, a, :, :],
+                in_=tok[6][:, 2 * a : 2 * a + 2, :, :].rearrange("p a q (b j) -> p q b a j", j=2),
                 axis=AXIS.XY,
                 op=ADD,
             )
@@ -234,24 +232,26 @@ def tile_apnb_pa_kernel(
             in1=ident[:, HEIGHT : 2 * HEIGHT].unsqueeze(1).to_broadcast([P, HEIGHT, WIDTH // 2]),
             op=ADD,
         )
-        nc.vector.tensor_copy(
-            out=where[:, PAIRS : PAIRS + P].rearrange("p (n two) -> p n two", two=2),
-            in_=where[:, PAIRS - P // 2 : PAIRS].unsqueeze(2).to_broadcast([P, P // 2, 2]),
-        )
         which = keep.tile([P, TOKENS], BF16)
+        member = {}
         for s in LEVELS:
-            member = keep.tile([P, 2, s], F32, name="member_%d" % s)
+            member[s] = keep.tile([P, 2, s], F32, name="member_%d" % s)
             nc.vector.tensor_reduce(
-                out=member[:],
+                out=member[s][:],
                 in_=ident[:, 0 : 2 * HEIGHT].rearrange("p (part a i) -> p part a i", part=2, a=s),
                 axis=AXIS.X,
                 op=ADD,
             )
+        nc.vector.tensor_copy(
+            out=where[:, PAIRS : PAIRS + P].rearrange("p (n two) -> p n two", two=2),
+            in_=where[:, PAIRS - P // 2 : PAIRS].unsqueeze(2).to_broadcast([P, P // 2, 2]),
+        )
+        for s in LEVELS:
             nc.vector.scalar_tensor_tensor(
                 out=which[:, first_token[s] : first_token[s] + s * s].rearrange("p (a b) -> p a b", b=s),
-                in0=member[:, 0, :].unsqueeze(2).to_broadcast([P, s, s]),
+                in0=member[s][:, 0, :].unsqueeze(2).to_broadcast([P, s, s]),
                 scalar=float(s * s) / 128.0,
-                in1=member[:, 1, :].unsqueeze(1).to_broadcast([P, s, s]),
+                in1=member[s][:, 1, :].unsqueeze(1).to_broadcast([P, s, s]),
                 op0=MULT,
                 op1=ADD,
             )
@@ -269,10 +269,10 @@ def tile_apnb_pa_kernel(
         ident_bf = keep.tile([P, P], BF16)
         nc.vector.tensor_copy(out=ident_bf[:], in_=ident[:])
         nc.vector.memset(pool_mat[:, :, TOKENS:P], 0.0)
-        pair = keep.tile([P, HALVES, PAIRS], F32)
+        pair = keep.tile([P, PAIRS, HALVES], F32)
         tok = {}
         for s in LEVELS:
-            tok[s] = keep.tile([P, HALVES, s * s], F32, name="tok_%d" % s)
+            tok[s] = keep.tile([P, s, HALVES, s], F32, name="tok_%d" % s)
         val = keep.tile([P, len(CHUNKS), HALVES * P], F32)
 
         val_01 = psum.tile([P, 2, HALVES * P], F32, tag="val_01")
@@ -285,8 +285,14 @@ def tile_apnb_pa_kernel(
 
         regroup(0, 0, nc.vector.tensor_copy)
         regroup(0, 1, nc.scalar.copy)
+        nc.vector.tensor_scalar(
+            out=pool_mat[:, LAST, 0:TOKENS], in0=hits_b[:, 0, :], scalar1=-1.0, scalar2=0.0, op0=ADD, op1=MAX
+        )
         quantise(0)
         project_val(0)
+        nc.vector.tensor_scalar(
+            out=pool_mat[:, 0:LAST, 0:TOKENS], in0=hits_a[:], scalar1=-1.0, scalar2=0.0, op0=ADD, op1=MAX
+        )
         regroup(1, 0, nc.vector.tensor_copy)
         regroup(1, 1, nc.scalar.copy)
         regroup(2, 0, nc.vector.tensor_copy)
@@ -299,11 +305,11 @@ def tile_apnb_pa_kernel(
         project_kf(1)
         regroup(3, 0, nc.vector.tensor_copy)
         regroup(3, 1, nc.scalar.copy)
-        per_ch = keep.tile([P, 10], F32)
-        nc.scalar.copy(out=per_ch[:], in_=vec_t[:, 0:10])
-        bk_c, gk_c, betak_c, mk_c, vk_c = [per_ch[:, 2 * v : 2 * v + 2] for v in range(5)]
         inv_std = keep.tile([P, 2], F32)
-        nc.scalar.activation(out=inv_std[:], in_=vk_c, func=ACT.Abs_reciprocal_sqrt, bias=EPS)
+        nc.scalar.activation(out=inv_std[:], in_=vec_t[:, 8:10], func=ACT.Abs_reciprocal_sqrt, bias=EPS)
+        per_ch = keep.tile([P, 8], F32)
+        nc.scalar.copy(out=per_ch[:], in_=vec_t[:, 0:8])
+        bk_c, gk_c, betak_c, mk_c = [per_ch[:, 2 * v : 2 * v + 2] for v in range(4)]
         quantise(2)
         project_val(2)
         project_kf(2)
@@ -311,13 +317,18 @@ def tile_apnb_pa_kernel(
         nc.vector.tensor_tensor(out=centred[:], in0=bk_c, in1=mk_c, op=SUBTRACT)
         gain = keep.tile([P, 2], F32)
         nc.vector.tensor_tensor(out=gain[:], in0=inv_std[:], in1=gk_c, op=MULT)
-        scaled = keep.tile([P, 2], F32)
-        nc.vector.tensor_tensor(out=scaled[:], in0=centred[:], in1=gain[:], op=MULT)
-        shift = keep.tile([P, 2], F32)
-        nc.vector.tensor_tensor(out=shift[:], in0=scaled[:], in1=betak_c, op=ADD)
         regroup(4, 0, nc.vector.tensor_copy)
         regroup(4, 1, nc.scalar.copy)
-        nc.scalar.activation(out=pool_mat[:, LAST, 0:TOKENS], in_=hits_b[:, 0, :], func=ACT.Relu, bias=-1.0)
+        shift = keep.tile([P, 2], F32)
+        for m in range(HALVES):
+            nc.vector.scalar_tensor_tensor(
+                out=shift[:, m : m + 1],
+                in0=centred[:, m : m + 1],
+                scalar=gain[:, m : m + 1],
+                in1=betak_c[:, m : m + 1],
+                op0=MULT,
+                op1=ADD,
+            )
         quantise(3)
         project_val(3)
         kf_acc[3] = psum.tile([P, HALVES, 2 * P], F32, tag="kf_3", name="kf_acc_3")
@@ -330,57 +341,81 @@ def tile_apnb_pa_kernel(
 
         keyp = keep.tile([P, HALVES, LEAD + TOKENS], F32)
 
-        def mean(s):
-            cells = slice(LEAD + first_token[s], LEAD + first_token[s] + s * s)
-            nc.scalar.mul(out=keyp[:, :, cells], in_=tok[s][:], mul=float(s * s) / POSITIONS)
+        def mean(s, a0, a1):
+            cells = slice(LEAD + first_token[s] + s * a0, LEAD + first_token[s] + s * a1)
+            nc.scalar.mul(
+                out=keyp[:, :, cells].rearrange("p q (a b) -> p q a b", b=s),
+                in_=tok[s][:, a0:a1, :, :].rearrange("p a q b -> p q a b"),
+                mul=float(s * s) / POSITIONS,
+            )
+
+        def mean_half(s, a0, a1, q):
+            cells = slice(LEAD + first_token[s] + s * a0, LEAD + first_token[s] + s * a1)
+            nc.scalar.mul(
+                out=keyp[:, q, cells].rearrange("p (a b) -> p a b", b=s),
+                in_=tok[s][:, a0:a1, q, :],
+                mul=float(s * s) / POSITIONS,
+            )
 
         norm_relu(0)
         add_pairs(0)
         norm_relu(1)
         add_pairs(1)
-        pool_cells(8, 0, 3)
-        nc.scalar.activation(out=pool_mat[:, 0:LAST, 0:TOKENS], in_=hits_a[:], func=ACT.Relu, bias=-1.0)
+        pool_row(6, 0)
         nc.scalar.copy(out=val[:, 0:2, :], in_=val_01[:])
         value_acc = psum.tile([P, HALVES * P], F32, tag="value")
         nc.tensor.matmul(out=value_acc[:], lhsT=nines_bf[:], rhs=bv_row[:], start=True, stop=False)
         pool_val(0, False)
         pool_val(1, False)
+        pool_rows(8, 0, 3, 0)
+        pool_row(6, 1)
+        pool_rows(8, 0, 3, 1)
         norm_relu(2)
-        pool_cells(6, 0, 2)
-        pool_level3(0)
         add_pairs(2)
+        pool_level3(0)
+        pool_row(6, 2)
+        pool_rows(8, 3, 5, 0)
+        pool_row(6, 3)
         norm_relu(3)
         add_pairs(3)
+        pool_rows(8, 3, 5, 1)
         nc.scalar.copy(out=val[:, 2:4, :], in_=val_23[:])
         pool_val(2, False)
         pool_val(3, False)
         norm_relu(4)
-        pool_cells(8, 3, 7)
-        pool_cells(6, 2, 5)
-        pool_level3(1)
+        pool_rows(8, 5, 7, 0)
+        pool_row(6, 4)
         nc.scalar.copy(out=val[:, 4, :], in_=val_acc[4])
         pool_val(4, True)
-
         add_pairs(4)
-        pool_cells(8, 7, 8)
+        pool_rows(8, 5, 7, 1)
+        pool_level3(1)
+        mean(6, 0, 5)
         value_sb = keep.tile([P, HALVES * P], F32)
         nc.scalar.mul(out=value_sb[:], in_=value_acc[:], mul=1.0 / 9.0)
         first_row = 0
         for rows in (64, 32, 8, 4, 2):
             nc.sync.dma_start(out=out_2[0, first_row : first_row + rows, :], in_=value_sb[first_row : first_row + rows, :])
             first_row += rows
-        edge = keep.tile([P, HALVES, LEAD], F32)
-        nc.scalar.mul(out=edge[:], in_=tok[8][:, :, 64 - LEAD : 64], mul=64.0 / POSITIONS)
-        before = psum.tile([P, HALVES, LEAD], F32, tag="kf_0")
-        nc.tensor.matmul(out=before[:], lhsT=down[:], rhs=edge[:], start=True, stop=True)
-        mean(8)
-        pool_cells(6, 5, 6)
-        mean(6)
+        mean(8, 0, 7)
+        pool_row(6, 5)
+        pool_row(8, 7)
         pool_level3(2)
-        mean(3)
-        nc.vector.tensor_reduce(out=tok[1][:, :, 0], in_=tok[3][:], axis=AXIS.X, op=ADD)
-        mean(1)
-        nc.scalar.copy(out=keyp[:, :, 0:LEAD], in_=before[:])
+        nc.vector.tensor_reduce(
+            out=tok[1][:, 0, :, 0], in_=tok[6][:].rearrange("p a q b -> p q a b"), axis=AXIS.XY, op=ADD
+        )
+        before = psum.tile([P, HALVES, LEAD], F32, tag="kf_0")
+        nc.tensor.matmul(out=before[:], lhsT=down[:], rhs=tok[8][:, 7, :, 8 - LEAD : 8], start=True, stop=True)
+        for q in range(HALVES):
+            mean_half(6, 5, 6, q)
+        for q in range(HALVES):
+            mean_half(8, 7, 8, q)
+        for q in range(HALVES):
+            mean_half(3, 0, 3, q)
+        for q in range(HALVES):
+            mean_half(1, 0, 1, q)
+        for q in range(HALVES):
+            nc.scalar.mul(out=keyp[:, q, 0:LEAD], in_=before[:, q, :], mul=64.0 / POSITIONS)
         groups = out_1[0].rearrange("(m q j) t -> q m (j t)", m=HALVES, j=4)
         for j in range(4):
             borrowed, lent = (-2 * j) % 8, (-2 * (j + 1)) % 8

@@ -186,22 +186,26 @@ def tile_apnb_pa_kernel(
 
         w_words = keep.tile([P, 2, GROUPS, 4 * P], U8, align_bytes=64)
         w_planes = keep.tile([P, 2, GROUPS, 2 * P], U8, align_bytes=64)
-        nc.vector.memset(w_planes[:].bitcast(I32), 0)
-        ident = keep.tile([P, P], F32)
-        make_identity(nc, ident[:])
         vec_rows = keep.tile([P, P], BF16)
-        nc.gpsimd.memset(vec_rows[:], 0.0)
-        down = keep.tile([P, P], F32)
-        nc.gpsimd.memset(down[:, 0:1], 0.0)
-        nc.gpsimd.tensor_copy(out=down[:, 1:P], in_=ident[:, 0 : P - 1])
+        nc.vector.memset(vec_rows[:], 0.0)
+        nc.vector.memset(w_planes[:].bitcast(I32), 0)
+        wide_ident = keep.tile([P, P + 1], F32)
+        nc.gpsimd.memset(wide_ident[:], 0.0)
+        ident = wide_ident[:, 1 : P + 1]
+        make_identity(nc, ident, nomemset=True)
+        down = wide_ident[:, 0:P]
         bv_row = keep.tile([P, HALVES * P], BF16)
-        nc.gpsimd.memset(bv_row[:], 0.0)
 
         def load_vector(queue, v, vec):
             queue.dma_start(out=vec_rows[2 * v : 2 * v + 2, :], in_=vec.rearrange("(m c) -> m c", m=2))
 
+        load_vector(nc.gpsimd, 4, vk)
+        load_vector(nc.gpsimd, 1, gk)
+        load_vector(nc.gpsimd, 2, betak)
         load(0, 1)
         load(0, 0)
+        load_vector(nc.sync, 0, bk)
+        load_vector(nc.sync, 3, mk)
         load(1, 1)
         load(1, 0)
         load_scales(1, Wv_scales)
@@ -209,21 +213,22 @@ def tile_apnb_pa_kernel(
         load(2, 1)
         load(2, 0)
         load_words(0, Wk_words)
-        load_vector(nc.sync, 0, bk)
-        load_vector(nc.sync, 3, mk)
         load_scales(0, Wk_scales)
         load(3, 1)
         load(3, 0)
-        nc.sync.dma_start(out=bv_row[0:1, :], in_=bv.rearrange("(o c) -> o c", o=1))
-        load_vector(nc.gpsimd, 4, vk)
-        load_vector(nc.gpsimd, 1, gk)
-        load_vector(nc.gpsimd, 2, betak)
 
         warm = keep.tile([P, 1], F32)
         nc.scalar.activation(out=warm[:], in_=ident[:, 0:1], func=ACT.Abs_reciprocal_sqrt, bias=1.0)
         pool_mat = keep.tile([P, len(CHUNKS), P], F32)
         nines_bf = keep.tile([P, P], BF16)
-        nc.gpsimd.memset(nines_bf[:], 9.0)
+        nc.scalar.activation(out=nines_bf[:], in_=ident, func=ACT.Copy, bias=9.0, scale=0.0)
+        nc.scalar.activation(
+            out=bv_row[:].rearrange("p (m c) -> p m c", m=HALVES),
+            in_=ident.unsqueeze(1).to_broadcast([P, HALVES, P]),
+            func=ACT.Copy,
+            scale=0.0,
+        )
+        nc.sync.dma_start(out=bv_row[0:1, :], in_=bv.rearrange("(o c) -> o c", o=1))
 
         where = keep.tile([P, PAIRS + P], BF16)
         nc.vector.tensor_tensor(
@@ -267,7 +272,7 @@ def tile_apnb_pa_kernel(
                 stop=True,
             )
         ident_bf = keep.tile([P, P], BF16)
-        nc.vector.tensor_copy(out=ident_bf[:], in_=ident[:])
+        nc.vector.tensor_copy(out=ident_bf[:], in_=ident)
         nc.vector.memset(pool_mat[:, :, TOKENS:P], 0.0)
         pair = keep.tile([P, PAIRS, HALVES], F32)
         tok = {}
@@ -297,28 +302,26 @@ def tile_apnb_pa_kernel(
         regroup(1, 1, nc.scalar.copy)
         regroup(2, 0, nc.vector.tensor_copy)
         regroup(2, 1, nc.scalar.copy)
-        quantise(1)
-        project_val(1)
         vec_t = psum.tile([P, P], BF16, tag="last")
         nc.tensor.transpose(vec_t[:], vec_rows[:], ident_bf[:])
-        project_kf(0)
-        project_kf(1)
-        regroup(3, 0, nc.vector.tensor_copy)
-        regroup(3, 1, nc.scalar.copy)
         inv_std = keep.tile([P, 2], F32)
         nc.scalar.activation(out=inv_std[:], in_=vec_t[:, 8:10], func=ACT.Abs_reciprocal_sqrt, bias=EPS)
         per_ch = keep.tile([P, 8], F32)
         nc.scalar.copy(out=per_ch[:], in_=vec_t[:, 0:8])
         bk_c, gk_c, betak_c, mk_c = [per_ch[:, 2 * v : 2 * v + 2] for v in range(4)]
-        quantise(2)
-        project_val(2)
-        project_kf(2)
+        quantise(1)
+        project_val(1)
+        project_kf(0)
+        project_kf(1)
+        regroup(3, 0, nc.vector.tensor_copy)
+        regroup(3, 1, nc.scalar.copy)
         centred = keep.tile([P, 2], F32)
         nc.vector.tensor_tensor(out=centred[:], in0=bk_c, in1=mk_c, op=SUBTRACT)
         gain = keep.tile([P, 2], F32)
         nc.vector.tensor_tensor(out=gain[:], in0=inv_std[:], in1=gk_c, op=MULT)
-        regroup(4, 0, nc.vector.tensor_copy)
-        regroup(4, 1, nc.scalar.copy)
+        quantise(2)
+        project_val(2)
+        project_kf(2)
         shift = keep.tile([P, 2], F32)
         for m in range(HALVES):
             nc.vector.scalar_tensor_tensor(
@@ -329,6 +332,8 @@ def tile_apnb_pa_kernel(
                 op0=MULT,
                 op1=ADD,
             )
+        regroup(4, 0, nc.vector.tensor_copy)
+        regroup(4, 1, nc.scalar.copy)
         quantise(3)
         project_val(3)
         kf_acc[3] = psum.tile([P, HALVES, 2 * P], F32, tag="kf_3", name="kf_acc_3")
@@ -405,7 +410,7 @@ def tile_apnb_pa_kernel(
             out=tok[1][:, 0, :, 0], in_=tok[6][:].rearrange("p a q b -> p q a b"), axis=AXIS.XY, op=ADD
         )
         before = psum.tile([P, HALVES, LEAD], F32, tag="kf_0")
-        nc.tensor.matmul(out=before[:], lhsT=down[:], rhs=tok[8][:, 7, :, 8 - LEAD : 8], start=True, stop=True)
+        nc.tensor.matmul(out=before[:], lhsT=down, rhs=tok[8][:, 7, :, 8 - LEAD : 8], start=True, stop=True)
         for q in range(HALVES):
             mean_half(6, 5, 6, q)
         for q in range(HALVES):

@@ -31,7 +31,7 @@ EPS = 1e-5
 LEAD = 6
 CHUNKS = ((0, 256), (256, 256), (512, 256), (768, 256), (1024, 128))
 LAST = len(CHUNKS) - 1
-LOADS = ((0, 256), (256, 512), (768, 256), (1024, 128))
+LOADS = ((0, 256), (256, 256), (512, 256), (768, 256), (1024, 128))
 
 FLOPS = 2 * 512 * 1024 * POSITIONS
 
@@ -71,17 +71,17 @@ def tile_apnb_pa_kernel(
                     in_=scales_in.bitcast(I32)[:, 4 * quad : 4 * quad + 4, :].rearrange("g r n -> r g n"),
                 )
 
-        def regroup(j, g, engine_copy):
+        def regroup(j, g, engine_copy, pars=slice(0, 2)):
             first, width = CHUNKS[j]
-            if g == 0:
+            if j not in grouped:
                 grouped[j] = keep.tile([P, GROUPS, width, PACK], BF16, name="grouped_%d" % j, align_bytes=64)
             which_load = [n for n, (lo, w) in enumerate(LOADS) if lo <= first and first + width <= lo + w][0]
             off = first - LOADS[which_load][0]
             src = raw[g, which_load][:, :, off : off + width]
             if j < LAST:
                 engine_copy(
-                    out=grouped[j][:, g].rearrange("p (par c i) t -> p par c t i", par=2, i=4),
-                    in_=src.rearrange("p t (c i par) -> p par c t i", par=2, i=4),
+                    out=grouped[j][:, g].rearrange("p (par c i) t -> p par c t i", par=2, i=4)[:, pars],
+                    in_=src.rearrange("p t (c i par) -> p par c t i", par=2, i=4)[:, pars],
                 )
             else:
                 engine_copy(
@@ -188,6 +188,8 @@ def tile_apnb_pa_kernel(
         w_planes = keep.tile([P, 2, GROUPS, 2 * P], U8, align_bytes=64)
         vec_rows = keep.tile([P, P], BF16)
         nc.vector.memset(vec_rows[:], 0.0)
+        zero = keep.tile([P, 1], F32)
+        nc.vector.memset(zero[:], 0.0)
         nc.vector.memset(w_planes[:].bitcast(I32), 0)
         wide_ident = keep.tile([P, P + 1], F32)
         nc.gpsimd.memset(wide_ident[:], 0.0)
@@ -208,17 +210,19 @@ def tile_apnb_pa_kernel(
         load_vector(nc.sync, 3, mk)
         load(1, 1)
         load(1, 0)
-        load_scales(1, Wv_scales)
-        load_words(1, Wv_words)
+        load_scales(0, Wk_scales)
+        load_words(0, Wk_words)
         load(2, 1)
         load(2, 0)
-        load_words(0, Wk_words)
-        load_scales(0, Wk_scales)
+        load_scales(1, Wv_scales)
+        load_words(1, Wv_words)
         load(3, 1)
         load(3, 0)
+        load(4, 1)
+        load(4, 0)
 
         warm = keep.tile([P, 1], F32)
-        nc.scalar.activation(out=warm[:], in_=ident[:, 0:1], func=ACT.Abs_reciprocal_sqrt, bias=1.0)
+        nc.scalar.activation(out=warm[:], in_=zero[:], func=ACT.Abs_reciprocal_sqrt, bias=1.0)
         pool_mat = keep.tile([P, len(CHUNKS), P], F32)
         nines_bf = keep.tile([P, P], BF16)
         nc.scalar.activation(out=nines_bf[:], in_=ident, func=ACT.Copy, bias=9.0, scale=0.0)
@@ -229,6 +233,9 @@ def tile_apnb_pa_kernel(
             scale=0.0,
         )
         nc.sync.dma_start(out=bv_row[0:1, :], in_=bv.rearrange("(o c) -> o c", o=1))
+
+        ident_bf = keep.tile([P, P], BF16)
+        nc.vector.tensor_copy(out=ident_bf[:], in_=ident)
 
         where = keep.tile([P, PAIRS + P], BF16)
         nc.vector.tensor_tensor(
@@ -271,8 +278,6 @@ def tile_apnb_pa_kernel(
                 start=True,
                 stop=True,
             )
-        ident_bf = keep.tile([P, P], BF16)
-        nc.vector.tensor_copy(out=ident_bf[:], in_=ident)
         nc.vector.memset(pool_mat[:, :, TOKENS:P], 0.0)
         pair = keep.tile([P, PAIRS, HALVES], F32)
         tok = {}
@@ -294,34 +299,36 @@ def tile_apnb_pa_kernel(
             out=pool_mat[:, LAST, 0:TOKENS], in0=hits_b[:, 0, :], scalar1=-1.0, scalar2=0.0, op0=ADD, op1=MAX
         )
         quantise(0)
-        project_val(0)
+        project_kf(0)
         nc.vector.tensor_scalar(
             out=pool_mat[:, 0:LAST, 0:TOKENS], in0=hits_a[:], scalar1=-1.0, scalar2=0.0, op0=ADD, op1=MAX
         )
-        regroup(1, 0, nc.vector.tensor_copy)
         regroup(1, 1, nc.scalar.copy)
-        regroup(2, 0, nc.vector.tensor_copy)
-        regroup(2, 1, nc.scalar.copy)
+        regroup(1, 0, nc.vector.tensor_copy)
+        quantise(1)
+        project_kf(1)
         vec_t = psum.tile([P, P], BF16, tag="last")
         nc.tensor.transpose(vec_t[:], vec_rows[:], ident_bf[:])
+        regroup(2, 1, nc.scalar.copy)
         inv_std = keep.tile([P, 2], F32)
         nc.scalar.activation(out=inv_std[:], in_=vec_t[:, 8:10], func=ACT.Abs_reciprocal_sqrt, bias=EPS)
         per_ch = keep.tile([P, 8], F32)
         nc.scalar.copy(out=per_ch[:], in_=vec_t[:, 0:8])
         bk_c, gk_c, betak_c, mk_c = [per_ch[:, 2 * v : 2 * v + 2] for v in range(4)]
-        quantise(1)
-        project_val(1)
-        project_kf(0)
-        project_kf(1)
-        regroup(3, 0, nc.vector.tensor_copy)
-        regroup(3, 1, nc.scalar.copy)
+        regroup(2, 0, nc.vector.tensor_copy)
+        quantise(2)
         centred = keep.tile([P, 2], F32)
         nc.vector.tensor_tensor(out=centred[:], in0=bk_c, in1=mk_c, op=SUBTRACT)
         gain = keep.tile([P, 2], F32)
         nc.vector.tensor_tensor(out=gain[:], in0=inv_std[:], in1=gk_c, op=MULT)
-        quantise(2)
-        project_val(2)
+        project_val(0)
+        project_val(1)
         project_kf(2)
+        project_val(2)
+        nc.scalar.copy(out=val[:, 0, :], in_=val_acc[0])
+        regroup(3, 1, nc.scalar.copy)
+        nc.vector.tensor_copy(out=val[:, 1, :], in_=val_acc[1])
+        regroup(3, 0, nc.vector.tensor_copy)
         shift = keep.tile([P, 2], F32)
         for m in range(HALVES):
             nc.vector.scalar_tensor_tensor(
@@ -332,18 +339,21 @@ def tile_apnb_pa_kernel(
                 op0=MULT,
                 op1=ADD,
             )
-        regroup(4, 0, nc.vector.tensor_copy)
-        regroup(4, 1, nc.scalar.copy)
+        value_acc = psum.tile([P, HALVES * P], F32, tag="value")
+        nc.tensor.matmul(out=value_acc[:], lhsT=nines_bf[:], rhs=bv_row[:], start=True, stop=False)
+        pool_val(0, False)
+        pool_val(1, False)
         quantise(3)
-        project_val(3)
         kf_acc[3] = psum.tile([P, HALVES, 2 * P], F32, tag="kf_3", name="kf_acc_3")
         project_kf(3)
+        project_val(3)
+        regroup(4, 1, nc.scalar.copy)
+        regroup(4, 0, nc.vector.tensor_copy)
         quantise(4)
         last = psum.tile([P, 4, P], F32, tag="last")
         kf_acc[4], val_acc[4] = last[:, 0:2, :], last[:, 2:4, :].rearrange("p a b -> p (a b)")
-        project_kf(4)
         project_val(4)
-
+        project_kf(4)
         keyp = keep.tile([P, HALVES, LEAD + TOKENS], F32)
 
         def mean(s, a0, a1):
@@ -363,45 +373,41 @@ def tile_apnb_pa_kernel(
             )
 
         norm_relu(0)
-        add_pairs(0)
         norm_relu(1)
+        add_pairs(0)
+        nc.scalar.copy(out=val[:, 2, :], in_=val_acc[2])
+        pool_val(2, False)
         add_pairs(1)
         pool_row(6, 0)
-        nc.scalar.copy(out=val[:, 0:2, :], in_=val_01[:])
-        value_acc = psum.tile([P, HALVES * P], F32, tag="value")
-        nc.tensor.matmul(out=value_acc[:], lhsT=nines_bf[:], rhs=bv_row[:], start=True, stop=False)
-        pool_val(0, False)
-        pool_val(1, False)
         pool_rows(8, 0, 3, 0)
         pool_row(6, 1)
         pool_rows(8, 0, 3, 1)
         norm_relu(2)
+        nc.scalar.copy(out=val[:, 3, :], in_=val_acc[3])
+        pool_val(3, False)
+        nc.scalar.copy(out=val[:, 4, :], in_=val_acc[4])
+        pool_val(4, True)
         add_pairs(2)
         pool_level3(0)
         pool_row(6, 2)
         pool_rows(8, 3, 5, 0)
         pool_row(6, 3)
         norm_relu(3)
+        norm_relu(4)
         add_pairs(3)
         pool_rows(8, 3, 5, 1)
-        nc.scalar.copy(out=val[:, 2:4, :], in_=val_23[:])
-        pool_val(2, False)
-        pool_val(3, False)
-        norm_relu(4)
         pool_rows(8, 5, 7, 0)
         pool_row(6, 4)
-        nc.scalar.copy(out=val[:, 4, :], in_=val_acc[4])
-        pool_val(4, True)
-        add_pairs(4)
-        pool_rows(8, 5, 7, 1)
-        pool_level3(1)
-        mean(6, 0, 5)
         value_sb = keep.tile([P, HALVES * P], F32)
         nc.scalar.mul(out=value_sb[:], in_=value_acc[:], mul=1.0 / 9.0)
         first_row = 0
         for rows in (64, 32, 8, 4, 2):
             nc.sync.dma_start(out=out_2[0, first_row : first_row + rows, :], in_=value_sb[first_row : first_row + rows, :])
             first_row += rows
+        add_pairs(4)
+        pool_rows(8, 5, 7, 1)
+        pool_level3(1)
+        mean(6, 0, 5)
         mean(8, 0, 7)
         pool_row(6, 5)
         pool_row(8, 7)

@@ -203,21 +203,21 @@ def tile_apnb_pa_kernel(
 
         load_vector(nc.gpsimd, 4, vk)
         load_vector(nc.gpsimd, 1, gk)
-        load_vector(nc.gpsimd, 2, betak)
         load(0, 1)
         load(0, 0)
         load_vector(nc.sync, 0, bk)
         load_vector(nc.sync, 3, mk)
+        load_vector(nc.sync, 2, betak)
         load(1, 1)
         load(1, 0)
-        load_scales(0, Wk_scales)
-        load_words(0, Wk_words)
         load(2, 1)
         load(2, 0)
         load_scales(1, Wv_scales)
         load_words(1, Wv_words)
         load(3, 1)
         load(3, 0)
+        load_words(0, Wk_words)
+        load_scales(0, Wk_scales)
         load(4, 1)
         load(4, 0)
 
@@ -299,16 +299,14 @@ def tile_apnb_pa_kernel(
             out=pool_mat[:, LAST, 0:TOKENS], in0=hits_b[:, 0, :], scalar1=-1.0, scalar2=0.0, op0=ADD, op1=MAX
         )
         quantise(0)
-        project_kf(0)
+        vec_t = psum.tile([P, P], BF16, tag="last")
+        nc.tensor.transpose(vec_t[:], vec_rows[:], ident_bf[:])
+        project_val(0)
+        regroup(1, 1, nc.scalar.copy)
+        regroup(1, 0, nc.vector.tensor_copy)
         nc.vector.tensor_scalar(
             out=pool_mat[:, 0:LAST, 0:TOKENS], in0=hits_a[:], scalar1=-1.0, scalar2=0.0, op0=ADD, op1=MAX
         )
-        regroup(1, 1, nc.scalar.copy)
-        regroup(1, 0, nc.vector.tensor_copy)
-        quantise(1)
-        project_kf(1)
-        vec_t = psum.tile([P, P], BF16, tag="last")
-        nc.tensor.transpose(vec_t[:], vec_rows[:], ident_bf[:])
         regroup(2, 1, nc.scalar.copy)
         inv_std = keep.tile([P, 2], F32)
         nc.scalar.activation(out=inv_std[:], in_=vec_t[:, 8:10], func=ACT.Abs_reciprocal_sqrt, bias=EPS)
@@ -316,18 +314,18 @@ def tile_apnb_pa_kernel(
         nc.scalar.copy(out=per_ch[:], in_=vec_t[:, 0:8])
         bk_c, gk_c, betak_c, mk_c = [per_ch[:, 2 * v : 2 * v + 2] for v in range(4)]
         regroup(2, 0, nc.vector.tensor_copy)
-        quantise(2)
+        quantise(1)
         centred = keep.tile([P, 2], F32)
         nc.vector.tensor_tensor(out=centred[:], in0=bk_c, in1=mk_c, op=SUBTRACT)
         gain = keep.tile([P, 2], F32)
         nc.vector.tensor_tensor(out=gain[:], in0=inv_std[:], in1=gk_c, op=MULT)
-        project_val(0)
         project_val(1)
-        project_kf(2)
+        project_kf(0)
+        project_kf(1)
+        quantise(2)
         project_val(2)
-        nc.scalar.copy(out=val[:, 0, :], in_=val_acc[0])
+        project_kf(2)
         regroup(3, 1, nc.scalar.copy)
-        nc.vector.tensor_copy(out=val[:, 1, :], in_=val_acc[1])
         regroup(3, 0, nc.vector.tensor_copy)
         shift = keep.tile([P, 2], F32)
         for m in range(HALVES):
@@ -339,21 +337,13 @@ def tile_apnb_pa_kernel(
                 op0=MULT,
                 op1=ADD,
             )
-        value_acc = psum.tile([P, HALVES * P], F32, tag="value")
-        nc.tensor.matmul(out=value_acc[:], lhsT=nines_bf[:], rhs=bv_row[:], start=True, stop=False)
-        pool_val(0, False)
-        pool_val(1, False)
+        regroup(4, 1, nc.scalar.copy)
         quantise(3)
         kf_acc[3] = psum.tile([P, HALVES, 2 * P], F32, tag="kf_3", name="kf_acc_3")
         project_kf(3)
         project_val(3)
-        regroup(4, 1, nc.scalar.copy)
+        norm_relu(0)
         regroup(4, 0, nc.vector.tensor_copy)
-        quantise(4)
-        last = psum.tile([P, 4, P], F32, tag="last")
-        kf_acc[4], val_acc[4] = last[:, 0:2, :], last[:, 2:4, :].rearrange("p a b -> p (a b)")
-        project_val(4)
-        project_kf(4)
         keyp = keep.tile([P, HALVES, LEAD + TOKENS], F32)
 
         def mean(s, a0, a1):
@@ -372,49 +362,55 @@ def tile_apnb_pa_kernel(
                 mul=float(s * s) / POSITIONS,
             )
 
-        norm_relu(0)
-        norm_relu(1)
         add_pairs(0)
-        nc.scalar.copy(out=val[:, 2, :], in_=val_acc[2])
-        pool_val(2, False)
+        norm_relu(1)
+        quantise(4)
+        last = psum.tile([P, 4, P], F32, tag="last")
+        kf_acc[4], val_acc[4] = last[:, 0:2, :], last[:, 2:4, :].rearrange("p a b -> p (a b)")
+        project_val(4)
+        project_kf(4)
         add_pairs(1)
         pool_row(6, 0)
+        nc.scalar.copy(out=val[:, 0:2, :], in_=val_01[:])
+        value_acc = psum.tile([P, HALVES * P], F32, tag="value")
+        nc.tensor.matmul(out=value_acc[:], lhsT=nines_bf[:], rhs=bv_row[:], start=True, stop=False)
+        pool_val(0, False)
+        pool_val(1, False)
         pool_rows(8, 0, 3, 0)
         pool_row(6, 1)
-        pool_rows(8, 0, 3, 1)
         norm_relu(2)
-        nc.scalar.copy(out=val[:, 3, :], in_=val_acc[3])
-        pool_val(3, False)
-        nc.scalar.copy(out=val[:, 4, :], in_=val_acc[4])
-        pool_val(4, True)
         add_pairs(2)
+        pool_rows(8, 0, 3, 1)
         pool_level3(0)
         pool_row(6, 2)
         pool_rows(8, 3, 5, 0)
         pool_row(6, 3)
+        nc.scalar.copy(out=val[:, 2:4, :], in_=val_23[:])
+        pool_val(2, False)
+        pool_val(3, False)
         norm_relu(3)
-        norm_relu(4)
         add_pairs(3)
         pool_rows(8, 3, 5, 1)
+        pool_level3(1)
+        norm_relu(4)
         pool_rows(8, 5, 7, 0)
         pool_row(6, 4)
+        nc.scalar.copy(out=val[:, 4, :], in_=val_acc[4])
+        pool_val(4, True)
+        add_pairs(4)
+        mean(6, 0, 5)
         value_sb = keep.tile([P, HALVES * P], F32)
         nc.scalar.mul(out=value_sb[:], in_=value_acc[:], mul=1.0 / 9.0)
-        first_row = 0
-        for rows in (64, 32, 8, 4, 2):
-            nc.sync.dma_start(out=out_2[0, first_row : first_row + rows, :], in_=value_sb[first_row : first_row + rows, :])
-            first_row += rows
-        add_pairs(4)
+        for lo, hi in ((0, 64), (64, 96), (96, TOKENS)):
+            nc.sync.dma_start(out=out_2[0, lo:hi, :], in_=value_sb[lo:hi, :])
         pool_rows(8, 5, 7, 1)
-        pool_level3(1)
-        mean(6, 0, 5)
         mean(8, 0, 7)
         pool_row(6, 5)
         pool_row(8, 7)
-        pool_level3(2)
         nc.vector.tensor_reduce(
             out=tok[1][:, 0, :, 0], in_=tok[6][:].rearrange("p a q b -> p q a b"), axis=AXIS.XY, op=ADD
         )
+        pool_level3(2)
         before = psum.tile([P, HALVES, LEAD], F32, tag="kf_0")
         nc.tensor.matmul(out=before[:], lhsT=down, rhs=tok[8][:, 7, :, 8 - LEAD : 8], start=True, stop=True)
         for q in range(HALVES):
@@ -422,9 +418,9 @@ def tile_apnb_pa_kernel(
         for q in range(HALVES):
             mean_half(8, 7, 8, q)
         for q in range(HALVES):
-            mean_half(3, 0, 3, q)
-        for q in range(HALVES):
             mean_half(1, 0, 1, q)
+        for q in range(HALVES):
+            mean_half(3, 0, 3, q)
         for q in range(HALVES):
             nc.scalar.mul(out=keyp[:, q, 0:LEAD], in_=before[:, q, :], mul=64.0 / POSITIONS)
         groups = out_1[0].rearrange("(m q j) t -> q m (j t)", m=HALVES, j=4)

@@ -299,10 +299,20 @@ def tile_apnb_pa_kernel(
             out=pool_mat[:, LAST, 0:TOKENS], in0=hits_b[:, 0, :], scalar1=-1.0, scalar2=0.0, op0=ADD, op1=MAX
         )
         quantise(0)
+        idle_bank = psum.tile([P, 4 * P], F32, tag="kf_2", name="idle_bank")
+        nc.tensor.matmul(out=idle_bank[:], lhsT=ident_bf[:], rhs=grouped[0][:, 0, 0:P, :].rearrange("p c t -> p (c t)"), start=True, stop=True)
+        regroup(1, 1, nc.scalar.copy)
+        for half in range(2):
+            nc.tensor.matmul(
+                out=idle_bank[:],
+                lhsT=ident_bf[:],
+                rhs=grouped[1][:, 1, half * P : (half + 1) * P, :].rearrange("p c t -> p (c t)"),
+                start=True,
+                stop=True,
+            )
         vec_t = psum.tile([P, P], BF16, tag="last")
         nc.tensor.transpose(vec_t[:], vec_rows[:], ident_bf[:])
         project_val(0)
-        regroup(1, 1, nc.scalar.copy)
         regroup(1, 0, nc.vector.tensor_copy)
         nc.vector.tensor_scalar(
             out=pool_mat[:, 0:LAST, 0:TOKENS], in0=hits_a[:], scalar1=-1.0, scalar2=0.0, op0=ADD, op1=MAX
@@ -344,6 +354,7 @@ def tile_apnb_pa_kernel(
         project_val(3)
         norm_relu(0)
         regroup(4, 0, nc.vector.tensor_copy)
+        quantise(4)
         keyp = keep.tile([P, HALVES, LEAD + TOKENS], F32)
 
         def mean(s, a0, a1):
@@ -364,7 +375,6 @@ def tile_apnb_pa_kernel(
 
         add_pairs(0)
         norm_relu(1)
-        quantise(4)
         last = psum.tile([P, 4, P], F32, tag="last")
         kf_acc[4], val_acc[4] = last[:, 0:2, :], last[:, 2:4, :].rearrange("p a b -> p (a b)")
         project_val(4)

@@ -212,12 +212,12 @@ def tile_apnb_pa_kernel(
         load(1, 0)
         load(2, 1)
         load(2, 0)
-        load_scales(1, Wv_scales)
-        load_words(1, Wv_words)
+        load_scales(0, Wk_scales)
+        load_words(0, Wk_words)
         load(3, 1)
         load(3, 0)
-        load_words(0, Wk_words)
-        load_scales(0, Wk_scales)
+        load_words(1, Wv_words)
+        load_scales(1, Wv_scales)
         load(4, 1)
         load(4, 0)
 
@@ -232,7 +232,7 @@ def tile_apnb_pa_kernel(
             func=ACT.Copy,
             scale=0.0,
         )
-        nc.sync.dma_start(out=bv_row[0:1, :], in_=bv.rearrange("(o c) -> o c", o=1))
+        nc.gpsimd.dma_start(out=bv_row[0:1, :], in_=bv.rearrange("(o c) -> o c", o=1))
 
         ident_bf = keep.tile([P, P], BF16)
         nc.vector.tensor_copy(out=ident_bf[:], in_=ident)
@@ -267,7 +267,7 @@ def tile_apnb_pa_kernel(
                 op0=MULT,
                 op1=ADD,
             )
-        hits_a = psum.tile([P, LAST, TOKENS], F32, tag="value")
+        hits_a = psum.tile([P, LAST, TOKENS], F32, tag="val_23")
         hits_b = psum.tile([P, 1, TOKENS], F32, tag="kf_3")
         for j in range(len(CHUNKS)):
             first = j * P if j < LAST else PAIRS
@@ -312,31 +312,25 @@ def tile_apnb_pa_kernel(
             )
         vec_t = psum.tile([P, P], BF16, tag="last")
         nc.tensor.transpose(vec_t[:], vec_rows[:], ident_bf[:])
-        project_val(0)
+        project_kf(0)
         regroup(1, 0, nc.vector.tensor_copy)
-        nc.vector.tensor_scalar(
-            out=pool_mat[:, 0:LAST, 0:TOKENS], in0=hits_a[:], scalar1=-1.0, scalar2=0.0, op0=ADD, op1=MAX
-        )
         regroup(2, 1, nc.scalar.copy)
         inv_std = keep.tile([P, 2], F32)
         nc.scalar.activation(out=inv_std[:], in_=vec_t[:, 8:10], func=ACT.Abs_reciprocal_sqrt, bias=EPS)
         per_ch = keep.tile([P, 8], F32)
         nc.scalar.copy(out=per_ch[:], in_=vec_t[:, 0:8])
         bk_c, gk_c, betak_c, mk_c = [per_ch[:, 2 * v : 2 * v + 2] for v in range(4)]
+        nc.scalar.activation(out=pool_mat[:, 0:LAST, 0:TOKENS], in_=hits_a[:], func=ACT.Relu, bias=-1.0)
         regroup(2, 0, nc.vector.tensor_copy)
         quantise(1)
         centred = keep.tile([P, 2], F32)
         nc.vector.tensor_tensor(out=centred[:], in0=bk_c, in1=mk_c, op=SUBTRACT)
         gain = keep.tile([P, 2], F32)
         nc.vector.tensor_tensor(out=gain[:], in0=inv_std[:], in1=gk_c, op=MULT)
-        project_val(1)
-        project_kf(0)
         project_kf(1)
+        value_acc = psum.tile([P, HALVES * P], F32, tag="value")
+        nc.tensor.matmul(out=value_acc[:], lhsT=nines_bf[:], rhs=bv_row[:], start=True, stop=False)
         quantise(2)
-        project_val(2)
-        project_kf(2)
-        regroup(3, 1, nc.scalar.copy)
-        regroup(3, 0, nc.vector.tensor_copy)
         shift = keep.tile([P, 2], F32)
         for m in range(HALVES):
             nc.vector.scalar_tensor_tensor(
@@ -347,14 +341,27 @@ def tile_apnb_pa_kernel(
                 op0=MULT,
                 op1=ADD,
             )
-        regroup(4, 1, nc.scalar.copy)
+        project_val(0)
+        project_val(1)
+        project_kf(2)
+        project_val(2)
+        regroup(3, 1, nc.scalar.copy)
+        regroup(3, 0, nc.vector.tensor_copy)
         quantise(3)
         kf_acc[3] = psum.tile([P, HALVES, 2 * P], F32, tag="kf_3", name="kf_acc_3")
         project_kf(3)
-        project_val(3)
         norm_relu(0)
+        regroup(4, 1, nc.scalar.copy)
+        add_pairs(0)
         regroup(4, 0, nc.vector.tensor_copy)
+        norm_relu(1)
+        pool_row(6, 0)
         quantise(4)
+        project_val(3)
+        last = psum.tile([P, 4, P], F32, tag="last")
+        kf_acc[4], val_acc[4] = last[:, 0:2, :], last[:, 2:4, :].rearrange("p a b -> p (a b)")
+        project_kf(4)
+        project_val(4)
         keyp = keep.tile([P, HALVES, LEAD + TOKENS], F32)
 
         def mean(s, a0, a1):
@@ -373,47 +380,35 @@ def tile_apnb_pa_kernel(
                 mul=float(s * s) / POSITIONS,
             )
 
-        add_pairs(0)
-        norm_relu(1)
-        last = psum.tile([P, 4, P], F32, tag="last")
-        kf_acc[4], val_acc[4] = last[:, 0:2, :], last[:, 2:4, :].rearrange("p a b -> p (a b)")
-        project_val(4)
-        project_kf(4)
         add_pairs(1)
-        pool_row(6, 0)
+        pool_row(8, 0)
+        pool_rows(8, 1, 3, 0)
         nc.scalar.copy(out=val[:, 0:2, :], in_=val_01[:])
-        value_acc = psum.tile([P, HALVES * P], F32, tag="value")
-        nc.tensor.matmul(out=value_acc[:], lhsT=nines_bf[:], rhs=bv_row[:], start=True, stop=False)
         pool_val(0, False)
         pool_val(1, False)
-        pool_rows(8, 0, 3, 0)
         pool_row(6, 1)
         norm_relu(2)
         add_pairs(2)
-        pool_rows(8, 0, 3, 1)
+        pool_rows(8, 1, 3, 1)
         pool_level3(0)
         pool_row(6, 2)
         pool_rows(8, 3, 5, 0)
         pool_row(6, 3)
-        nc.scalar.copy(out=val[:, 2:4, :], in_=val_23[:])
-        pool_val(2, False)
-        pool_val(3, False)
         norm_relu(3)
         add_pairs(3)
         pool_rows(8, 3, 5, 1)
         pool_level3(1)
+        nc.scalar.copy(out=val[:, 2:4, :], in_=val_23[:])
+        pool_val(2, False)
+        pool_val(3, False)
         norm_relu(4)
         pool_rows(8, 5, 7, 0)
         pool_row(6, 4)
         nc.scalar.copy(out=val[:, 4, :], in_=val_acc[4])
-        pool_val(4, True)
         add_pairs(4)
         mean(6, 0, 5)
-        value_sb = keep.tile([P, HALVES * P], F32)
-        nc.scalar.mul(out=value_sb[:], in_=value_acc[:], mul=1.0 / 9.0)
-        for lo, hi in ((0, 64), (64, 96), (96, TOKENS)):
-            nc.sync.dma_start(out=out_2[0, lo:hi, :], in_=value_sb[lo:hi, :])
         pool_rows(8, 5, 7, 1)
+        pool_val(4, True)
         mean(8, 0, 7)
         pool_row(6, 5)
         pool_row(8, 7)
@@ -433,12 +428,15 @@ def tile_apnb_pa_kernel(
             mean_half(3, 0, 3, q)
         for q in range(HALVES):
             nc.scalar.mul(out=keyp[:, q, 0:LEAD], in_=before[:, q, :], mul=64.0 / POSITIONS)
+        value_sb = keep.tile([P, HALVES * P], F32)
+        nc.vector.tensor_scalar(out=value_sb[:], in0=value_acc[:], scalar1=1.0 / 9.0, scalar2=None, op0=MULT)
         groups = out_1[0].rearrange("(m q j) t -> q m (j t)", m=HALVES, j=4)
         for j in range(4):
             borrowed, lent = (-2 * j) % 8, (-2 * (j + 1)) % 8
             length = borrowed + TOKENS - lent
-            queue = nc.sync if j % 2 == 0 else nc.scalar
-            queue.dma_start(
+            nc.scalar.dma_start(
                 out=groups[:, :, TOKENS * j - borrowed : TOKENS * j - borrowed + length],
                 in_=keyp[j:P:4, :, LEAD - borrowed : LEAD - borrowed + length],
             )
+        for lo, hi in ((0, 64), (64, 96), (96, TOKENS)):
+            nc.sync.dma_start(out=out_2[0, lo:hi, :], in_=value_sb[lo:hi, :])

@@ -232,7 +232,7 @@ def tile_apnb_pa_kernel(
             func=ACT.Copy,
             scale=0.0,
         )
-        nc.gpsimd.dma_start(out=bv_row[0:1, :], in_=bv.rearrange("(o c) -> o c", o=1))
+        nc.sync.dma_start(out=bv_row[0:1, :], in_=bv.rearrange("(o c) -> o c", o=1))
 
         ident_bf = keep.tile([P, P], BF16)
         nc.vector.tensor_copy(out=ident_bf[:], in_=ident)
@@ -300,16 +300,22 @@ def tile_apnb_pa_kernel(
         )
         quantise(0)
         idle_bank = psum.tile([P, 4 * P], F32, tag="kf_2", name="idle_bank")
-        nc.tensor.matmul(out=idle_bank[:], lhsT=ident_bf[:], rhs=grouped[0][:, 0, 0:P, :].rearrange("p c t -> p (c t)"), start=True, stop=True)
-        regroup(1, 1, nc.scalar.copy)
         for half in range(2):
             nc.tensor.matmul(
                 out=idle_bank[:],
                 lhsT=ident_bf[:],
-                rhs=grouped[1][:, 1, half * P : (half + 1) * P, :].rearrange("p c t -> p (c t)"),
+                rhs=grouped[0][:, 0, half * P : (half + 1) * P, :].rearrange("p c t -> p (c t)"),
                 start=True,
                 stop=True,
             )
+        regroup(1, 1, nc.scalar.copy)
+        nc.tensor.matmul(
+            out=idle_bank[:],
+            lhsT=ident_bf[:],
+            rhs=grouped[1][:, 1, 0:P, :].rearrange("p c t -> p (c t)"),
+            start=True,
+            stop=True,
+        )
         vec_t = psum.tile([P, P], BF16, tag="last")
         nc.tensor.transpose(vec_t[:], vec_rows[:], ident_bf[:])
         project_kf(0)
@@ -328,8 +334,6 @@ def tile_apnb_pa_kernel(
         gain = keep.tile([P, 2], F32)
         nc.vector.tensor_tensor(out=gain[:], in0=inv_std[:], in1=gk_c, op=MULT)
         project_kf(1)
-        value_acc = psum.tile([P, HALVES * P], F32, tag="value")
-        nc.tensor.matmul(out=value_acc[:], lhsT=nines_bf[:], rhs=bv_row[:], start=True, stop=False)
         quantise(2)
         shift = keep.tile([P, 2], F32)
         for m in range(HALVES):
@@ -384,6 +388,8 @@ def tile_apnb_pa_kernel(
         pool_row(8, 0)
         pool_rows(8, 1, 3, 0)
         nc.scalar.copy(out=val[:, 0:2, :], in_=val_01[:])
+        value_acc = psum.tile([P, HALVES * P], F32, tag="value")
+        nc.tensor.matmul(out=value_acc[:], lhsT=nines_bf[:], rhs=bv_row[:], start=True, stop=False)
         pool_val(0, False)
         pool_val(1, False)
         pool_row(6, 1)

@@ -345,9 +345,9 @@ def tile_apnb_pa_kernel(
                 op0=MULT,
                 op1=ADD,
             )
+        project_kf(2)
         project_val(0)
         project_val(1)
-        project_kf(2)
         project_val(2)
         regroup(3, 1, nc.scalar.copy)
         regroup(3, 0, nc.vector.tensor_copy)
@@ -409,31 +409,31 @@ def tile_apnb_pa_kernel(
         pool_val(3, False)
         norm_relu(4)
         pool_rows(8, 5, 7, 0)
-        pool_row(6, 4)
         nc.scalar.copy(out=val[:, 4, :], in_=val_acc[4])
         add_pairs(4)
+        pool_row(6, 4)
+        pool_row(8, 7)
         mean(6, 0, 5)
+        pool_row(6, 5)
         pool_rows(8, 5, 7, 1)
         pool_val(4, True)
-        mean(8, 0, 7)
-        pool_row(6, 5)
-        pool_row(8, 7)
-        nc.vector.tensor_reduce(
-            out=tok[1][:, 0, :, 0], in_=tok[6][:].rearrange("p a q b -> p q a b"), axis=AXIS.XY, op=ADD
-        )
-        pool_level3(2)
         before = psum.tile([P, HALVES, LEAD], F32, tag="kf_0")
         nc.tensor.matmul(out=before[:], lhsT=down, rhs=tok[8][:, 7, :, 8 - LEAD : 8], start=True, stop=True)
         for q in range(HALVES):
-            mean_half(6, 5, 6, q)
-        for q in range(HALVES):
             mean_half(8, 7, 8, q)
+        for q in range(HALVES):
+            mean_half(6, 5, 6, q)
+        nc.vector.tensor_reduce(
+            out=tok[1][:, 0, :, 0], in_=tok[6][:].rearrange("p a q b -> p q a b"), axis=AXIS.XY, op=ADD
+        )
+        mean(8, 0, 7)
+        pool_level3(2)
+        for q in range(HALVES):
+            nc.scalar.mul(out=keyp[:, q, 0:LEAD], in_=before[:, q, :], mul=64.0 / POSITIONS)
         for q in range(HALVES):
             mean_half(1, 0, 1, q)
         for q in range(HALVES):
             mean_half(3, 0, 3, q)
-        for q in range(HALVES):
-            nc.scalar.mul(out=keyp[:, q, 0:LEAD], in_=before[:, q, :], mul=64.0 / POSITIONS)
         value_sb = keep.tile([P, HALVES * P], F32)
         nc.vector.tensor_scalar(out=value_sb[:], in0=value_acc[:], scalar1=1.0 / 9.0, scalar2=None, op0=MULT)
         groups = out_1[0].rearrange("(m q j) t -> q m (j t)", m=HALVES, j=4)
@@ -444,5 +444,5 @@ def tile_apnb_pa_kernel(
                 out=groups[:, :, TOKENS * j - borrowed : TOKENS * j - borrowed + length],
                 in_=keyp[j:P:4, :, LEAD - borrowed : LEAD - borrowed + length],
             )
-        for lo, hi in ((0, 64), (64, 96), (96, TOKENS)):
+        for lo, hi in ((96, TOKENS), (0, 64), (64, 96)):
             nc.sync.dma_start(out=out_2[0, lo:hi, :], in_=value_sb[lo:hi, :])

@@ -188,6 +188,8 @@ def tile_apnb_pa_kernel(
         w_planes = keep.tile([P, 2, GROUPS, 2 * P], U8, align_bytes=64)
         vec_rows = keep.tile([P, P], BF16)
         nc.vector.memset(vec_rows[:], 0.0)
+        bv_row = keep.tile([P, HALVES * P], BF16)
+        nc.vector.memset(bv_row[:], 0.0)
         zero = keep.tile([P, 1], F32)
         nc.vector.memset(zero[:], 0.0)
         nc.vector.memset(w_planes[:].bitcast(I32), 0)
@@ -196,7 +198,6 @@ def tile_apnb_pa_kernel(
         ident = wide_ident[:, 1 : P + 1]
         make_identity(nc, ident, nomemset=True)
         down = wide_ident[:, 0:P]
-        bv_row = keep.tile([P, HALVES * P], BF16)
 
         def load_vector(queue, v, vec):
             queue.dma_start(out=vec_rows[2 * v : 2 * v + 2, :], in_=vec.rearrange("(m c) -> m c", m=2))
@@ -208,6 +209,7 @@ def tile_apnb_pa_kernel(
         load_vector(nc.sync, 0, bk)
         load_vector(nc.sync, 3, mk)
         load_vector(nc.sync, 2, betak)
+        nc.sync.dma_start(out=bv_row[0:1, :], in_=bv.rearrange("(o c) -> o c", o=1))
         load(1, 1)
         load(1, 0)
         load(2, 1)
@@ -226,13 +228,6 @@ def tile_apnb_pa_kernel(
         pool_mat = keep.tile([P, len(CHUNKS), P], F32)
         nines_bf = keep.tile([P, P], BF16)
         nc.scalar.activation(out=nines_bf[:], in_=ident, func=ACT.Copy, bias=9.0, scale=0.0)
-        nc.scalar.activation(
-            out=bv_row[:].rearrange("p (m c) -> p m c", m=HALVES),
-            in_=ident.unsqueeze(1).to_broadcast([P, HALVES, P]),
-            func=ACT.Copy,
-            scale=0.0,
-        )
-        nc.sync.dma_start(out=bv_row[0:1, :], in_=bv.rearrange("(o c) -> o c", o=1))
 
         ident_bf = keep.tile([P, P], BF16)
         nc.vector.tensor_copy(out=ident_bf[:], in_=ident)
@@ -318,6 +313,8 @@ def tile_apnb_pa_kernel(
         )
         vec_t = psum.tile([P, P], BF16, tag="last")
         nc.tensor.transpose(vec_t[:], vec_rows[:], ident_bf[:])
+        value_acc = psum.tile([P, HALVES * P], F32, tag="value")
+        nc.tensor.matmul(out=value_acc[:], lhsT=nines_bf[:], rhs=bv_row[:], start=True, stop=False)
         project_kf(0)
         regroup(1, 0, nc.vector.tensor_copy)
         regroup(2, 1, nc.scalar.copy)
@@ -327,8 +324,8 @@ def tile_apnb_pa_kernel(
         nc.scalar.copy(out=per_ch[:], in_=vec_t[:, 0:8])
         bk_c, gk_c, betak_c, mk_c = [per_ch[:, 2 * v : 2 * v + 2] for v in range(4)]
         nc.scalar.activation(out=pool_mat[:, 0:LAST, 0:TOKENS], in_=hits_a[:], func=ACT.Relu, bias=-1.0)
-        regroup(2, 0, nc.vector.tensor_copy)
         quantise(1)
+        regroup(2, 0, nc.vector.tensor_copy)
         centred = keep.tile([P, 2], F32)
         nc.vector.tensor_tensor(out=centred[:], in0=bk_c, in1=mk_c, op=SUBTRACT)
         gain = keep.tile([P, 2], F32)
@@ -388,8 +385,6 @@ def tile_apnb_pa_kernel(
         pool_row(8, 0)
         pool_rows(8, 1, 3, 0)
         nc.scalar.copy(out=val[:, 0:2, :], in_=val_01[:])
-        value_acc = psum.tile([P, HALVES * P], F32, tag="value")
-        nc.tensor.matmul(out=value_acc[:], lhsT=nines_bf[:], rhs=bv_row[:], start=True, stop=False)
         pool_val(0, False)
         pool_val(1, False)
         pool_row(6, 1)

@@ -89,14 +89,16 @@ def tile_apnb_pa_kernel(
                     in_=src.rearrange("p t (c i) -> p c t i", i=4),
                 )
 
-        def quantise(j):
+        def quantise(j, groups=slice(0, GROUPS)):
             width = CHUNKS[j][1]
-            codes[j] = keep.tile([P, GROUPS * width], U32, name="codes_%d" % j, align_bytes=64)
-            scales[j] = keep.tile([P, GROUPS * width], U8, name="scales_%d" % j, align_bytes=64)
+            if j not in codes:
+                codes[j] = keep.tile([P, GROUPS * width], U32, name="codes_%d" % j, align_bytes=64)
+                scales[j] = keep.tile([P, GROUPS * width], U8, name="scales_%d" % j, align_bytes=64)
+            cols = slice(groups.start * width, groups.stop * width)
             nc.vector.quantize_mx(
-                out=codes[j][:].bitcast(FP8X4),
-                scales=scales[j][:],
-                in_=grouped[j][:].rearrange("p g c t -> p (g c t)"),
+                out=codes[j][:, cols].bitcast(FP8X4),
+                scales=scales[j][:, cols],
+                in_=grouped[j][:, groups].rearrange("p g c t -> p (g c t)"),
             )
 
         def project_val(j):
@@ -324,14 +326,16 @@ def tile_apnb_pa_kernel(
         nc.scalar.copy(out=per_ch[:], in_=vec_t[:, 0:8])
         bk_c, gk_c, betak_c, mk_c = [per_ch[:, 2 * v : 2 * v + 2] for v in range(4)]
         nc.scalar.activation(out=pool_mat[:, 0:LAST, 0:TOKENS], in_=hits_a[:], func=ACT.Relu, bias=-1.0)
-        quantise(1)
+        quantise(1, slice(1, 2))
+        quantise(1, slice(0, 1))
+        project_kf(1)
         regroup(2, 0, nc.vector.tensor_copy)
+        quantise(2, slice(1, 2))
         centred = keep.tile([P, 2], F32)
         nc.vector.tensor_tensor(out=centred[:], in0=bk_c, in1=mk_c, op=SUBTRACT)
         gain = keep.tile([P, 2], F32)
         nc.vector.tensor_tensor(out=gain[:], in0=inv_std[:], in1=gk_c, op=MULT)
-        project_kf(1)
-        quantise(2)
+        quantise(2, slice(0, 1))
         shift = keep.tile([P, 2], F32)
         for m in range(HALVES):
             nc.vector.scalar_tensor_tensor(
@@ -348,7 +352,8 @@ def tile_apnb_pa_kernel(
         project_val(2)
         regroup(3, 1, nc.scalar.copy)
         regroup(3, 0, nc.vector.tensor_copy)
-        quantise(3)
+        quantise(3, slice(1, 2))
+        quantise(3, slice(0, 1))
         kf_acc[3] = psum.tile([P, HALVES, 2 * P], F32, tag="kf_3", name="kf_acc_3")
         project_kf(3)
         norm_relu(0)

from contextlib import ExitStack

import concourse.mybir as mybir
from concourse.masks import make_identity

BF16 = mybir.dt.bfloat16
F32 = mybir.dt.float32
I32 = mybir.dt.int32
U8 = mybir.dt.uint8
U32 = mybir.dt.uint32
FP8X4 = mybir.dt.float8_e4m3fn_x4
FP4X4 = mybir.dt.float4_e2m1fn_x4
ADD = mybir.AluOpType.add
MULT = mybir.AluOpType.mult
SUBTRACT = mybir.AluOpType.subtract
MAX = mybir.AluOpType.max
ACT = mybir.ActivationFunctionType
AXIS = mybir.AxisListType

P = 128
PACK = 4
GROUPS = 2
HEIGHT = 24
WIDTH = 48
POSITIONS = HEIGHT * WIDTH
PAIRS = POSITIONS // 2
HALVES = 2
LEVELS = (1, 3, 6, 8)
TOKENS = 110
EPS = 1e-5
LEAD = 6
CHUNKS = ((0, 256), (256, 256), (512, 256), (768, 256), (1024, 128))
LAST = len(CHUNKS) - 1
LOADS = ((0, 256), (256, 256), (512, 256), (768, 256), (1024, 128))

FLOPS = 2 * 512 * 1024 * POSITIONS


def tile_apnb_pa_kernel(
    tc, feats, Wk_words, Wk_scales, bk, gk, betak, mk, vk, Wv_words, Wv_scales, bv, out_0, out_1, out_2
):
    nc = tc.nc
    first_token = {1: 0, 3: 1, 6: 10, 8: 46}
    with ExitStack() as ctx:
        keep = ctx.enter_context(tc.tile_pool(name="keep", bufs=1))
        psum = ctx.enter_context(tc.psum_pool(name="psum", bufs=1))
        ctx.enter_context(tc.manual_schedule())

        x_rows = feats[0].rearrange("(g p t) h w -> g p t (h w)", p=P, t=PACK)
        kf_out = out_0[0].rearrange("(m p) h w -> p m (h w)", p=P)
        raw = {}
        grouped = {}
        codes = {}
        scales = {}
        kf_acc = {}
        val_acc = {}
        kf = {}

        def load(which_load, g):
            first, width = LOADS[which_load]
            raw[g, which_load] = keep.tile([P, PACK, width], BF16, name="raw_%d_%d" % (g, which_load))
            nc.sync.dma_start(out=raw[g, which_load][:], in_=x_rows[g, :, :, first : first + width])

        def load_words(wt, words):
            nc.sync.dma_start(out=w_words[:, wt].bitcast(I32), in_=words.bitcast(I32).rearrange("g p n -> p g n"))

        def load_scales(wt, scales_in):
            for quad in range(4):
                nc.sync.dma_start(
                    out=w_planes[32 * quad : 32 * quad + 4, wt].bitcast(I32),
                    in_=scales_in.bitcast(I32)[:, 4 * quad : 4 * quad + 4, :].rearrange("g r n -> r g n"),
                )

        def regroup(j, g, engine_copy, pars=slice(0, 2)):
            first, width = CHUNKS[j]
            if j not in grouped:
                grouped[j] = keep.tile([P, GROUPS, width, PACK], BF16, name="grouped_%d" % j, align_bytes=64)
            which_load = [n for n, (lo, w) in enumerate(LOADS) if lo <= first and first + width <= lo + w][0]
            off = first - LOADS[which_load][0]
            src = raw[g, which_load][:, :, off : off + width]
            if j < LAST:
                engine_copy(
                    out=grouped[j][:, g].rearrange("p (par c i) t -> p par c t i", par=2, i=4)[:, pars],
                    in_=src.rearrange("p t (c i par) -> p par c t i", par=2, i=4)[:, pars],
                )
            else:
                engine_copy(
                    out=grouped[j][:, g].rearrange("p (c i) t -> p c t i", i=4),
                    in_=src.rearrange("p t (c i) -> p c t i", i=4),
                )

        def quantise(j, groups=slice(0, GROUPS)):
            width = CHUNKS[j][1]
            if j not in codes:
                codes[j] = keep.tile([P, GROUPS * width], U32, name="codes_%d" % j, align_bytes=64)
                scales[j] = keep.tile([P, GROUPS * width], U8, name="scales_%d" % j, align_bytes=64)
            cols = slice(groups.start * width, groups.stop * width)
            nc.vector.quantize_mx(
                out=codes[j][:, cols].bitcast(FP8X4),
                scales=scales[j][:, cols],
                in_=grouped[j][:, groups].rearrange("p g c t -> p (g c t)"),
            )

        def project_val(j):
            width = CHUNKS[j][1]
            slices = [(g, s) for s in range(width // P) for g in range(GROUPS)]
            for m in range(HALVES):
                for n, (g, s) in enumerate(slices):
                    cols = slice(g * width + s * P, g * width + (s + 1) * P)
                    nc.tensor.matmul_mx(
                        out=val_acc[j][:, m * P : (m + 1) * P],
                        lhsT=codes[j][:, cols].bitcast(FP8X4),
                        lhsT_scale=scales[j][:, cols],
                        rhs=w_words[:, 1, g, 2 * P * m : 2 * P * (m + 1)].bitcast(FP4X4),
                        rhs_scale=w_planes[:, 1, g, P * m : P * (m + 1)],
                        start=(n == 0),
                        stop=(n == len(slices) - 1),
                    )

        def project_kf(j):
            width = CHUNKS[j][1]
            for m in range(HALVES):
                for s in range(width // P):
                    for g in range(GROUPS):
                        cols = slice(g * width + s * P, g * width + (s + 1) * P)
                        nc.tensor.matmul_mx(
                            out=kf_acc[j][:, m, s * P : (s + 1) * P],
                            lhsT=w_words[:, 0, g, 2 * P * m : 2 * P * (m + 1)].bitcast(FP4X4),
                            lhsT_scale=w_planes[:, 0, g, P * m : P * (m + 1)],
                            rhs=codes[j][:, cols].bitcast(FP8X4),
                            rhs_scale=scales[j][:, cols],
                            start=(g == 0),
                            stop=(g == GROUPS - 1),
                        )

        def norm_relu(j):
            first, width = CHUNKS[j]
            kf[j] = keep.tile([P, HALVES, width], F32, name="kf_%d" % j)
            for m in range(HALVES):
                if j < LAST:
                    out = kf[j][:, m, :].rearrange("p (u par) -> p u par", par=2)
                    in_ = kf_acc[j][:, m, :].rearrange("p (par u) -> p u par", par=2)
                else:
                    out = kf[j][:, m, :]
                    in_ = kf_acc[j][:, m, :]
                nc.scalar.activation(
                    out=out, in_=in_, func=ACT.Relu, bias=shift[:, m : m + 1], scale=gain[:, m : m + 1]
                )
            nc.sync.dma_start(out=kf_out[:, :, first : first + width], in_=kf[j][:])

        def pool_val(j, stop):
            nc.tensor.matmul(out=value_acc[:], lhsT=pool_mat[:, j, :], rhs=val[:, j, :], start=False, stop=stop)

        def add_pairs(j):
            first, width = CHUNKS[j]
            halves = kf[j][:].rearrange("p q (n two) -> p n q two", two=2)
            nc.vector.tensor_tensor(
                out=pair[:, first // 2 : (first + width) // 2, :], in0=halves[:, :, :, 0], in1=halves[:, :, :, 1], op=ADD
            )

        def pool_row(s, a):
            rows, wide = HEIGHT // s, WIDTH // 2 // s
            per = rows * (WIDTH // 2)
            nc.vector.tensor_reduce(
                out=tok[s][:, a, :, :],
                in_=pair[:, per * a : per * (a + 1), :].rearrange("p (i b j) q -> p q b i j", i=rows, b=s, j=wide),
                axis=AXIS.XY,
                op=ADD,
            )

        def pool_rows(s, a0, a1, q):
            rows, wide = HEIGHT // s, WIDTH // 2 // s
            per = rows * (WIDTH // 2)
            nc.vector.tensor_reduce(
                out=tok[s][:, a0:a1, q, :],
                in_=pair[:, per * a0 : per * a1, q].rearrange("p (a i b j) -> p a b i j", i=rows, b=s, j=wide),
                axis=AXIS.XY,
                op=ADD,
            )

        def pool_level3(a):
            nc.vector.tensor_reduce(
                out=tok[3][:, a, :, :],
                in_=tok[6][:, 2 * a : 2 * a + 2, :, :].rearrange("p a q (b j) -> p q b a j", j=2),
                axis=AXIS.XY,
                op=ADD,
            )

        w_words = keep.tile([P, 2, GROUPS, 4 * P], U8, align_bytes=64)
        w_planes = keep.tile([P, 2, GROUPS, 2 * P], U8, align_bytes=64)
        vec_rows = keep.tile([P, P], BF16)
        nc.vector.memset(vec_rows[:], 0.0)
        bv_row = keep.tile([P, HALVES * P], BF16)
        nc.vector.memset(bv_row[:], 0.0)
        zero = keep.tile([P, 1], F32)
        nc.vector.memset(zero[:], 0.0)
        nc.vector.memset(w_planes[:].bitcast(I32), 0)
        wide_ident = keep.tile([P, P + 1], F32)
        nc.gpsimd.memset(wide_ident[:], 0.0)
        ident = wide_ident[:, 1 : P + 1]
        make_identity(nc, ident, nomemset=True)
        down = wide_ident[:, 0:P]

        def load_vector(queue, v, vec):
            queue.dma_start(out=vec_rows[2 * v : 2 * v + 2, :], in_=vec.rearrange("(m c) -> m c", m=2))

        load_vector(nc.gpsimd, 4, vk)
        load_vector(nc.gpsimd, 1, gk)
        load(0, 1)
        load(0, 0)
        load_vector(nc.sync, 0, bk)
        load_vector(nc.sync, 3, mk)
        load_vector(nc.sync, 2, betak)
        nc.sync.dma_start(out=bv_row[0:1, :], in_=bv.rearrange("(o c) -> o c", o=1))
        load(1, 1)
        load(1, 0)
        load(2, 1)
        load(2, 0)
        load_scales(0, Wk_scales)
        load_words(0, Wk_words)
        load(3, 1)
        load(3, 0)
        load_words(1, Wv_words)
        load_scales(1, Wv_scales)
        load(4, 1)
        load(4, 0)

        warm = keep.tile([P, 1], F32)
        nc.scalar.activation(out=warm[:], in_=zero[:], func=ACT.Abs_reciprocal_sqrt, bias=1.0)
        pool_mat = keep.tile([P, len(CHUNKS), P], F32)
        nines_bf = keep.tile([P, P], BF16)
        nc.scalar.activation(out=nines_bf[:], in_=ident, func=ACT.Copy, bias=9.0, scale=0.0)

        ident_bf = keep.tile([P, P], BF16)
        nc.vector.tensor_copy(out=ident_bf[:], in_=ident)

        where = keep.tile([P, PAIRS + P], BF16)
        nc.vector.tensor_tensor(
            out=where[:, 0:PAIRS].rearrange("p (h c) -> p h c", h=HEIGHT),
            in0=ident[:, 0:HEIGHT].unsqueeze(2).to_broadcast([P, HEIGHT, WIDTH // 2]),
            in1=ident[:, HEIGHT : 2 * HEIGHT].unsqueeze(1).to_broadcast([P, HEIGHT, WIDTH // 2]),
            op=ADD,
        )
        which = keep.tile([P, TOKENS], BF16)
        member = {}
        for s in LEVELS:
            member[s] = keep.tile([P, 2, s], F32, name="member_%d" % s)
            nc.vector.tensor_reduce(
                out=member[s][:],
                in_=ident[:, 0 : 2 * HEIGHT].rearrange("p (part a i) -> p part a i", part=2, a=s),
                axis=AXIS.X,
                op=ADD,
            )
        nc.vector.tensor_copy(
            out=where[:, PAIRS : PAIRS + P].rearrange("p (n two) -> p n two", two=2),
            in_=where[:, PAIRS - P // 2 : PAIRS].unsqueeze(2).to_broadcast([P, P // 2, 2]),
        )
        for s in LEVELS:
            nc.vector.scalar_tensor_tensor(
                out=which[:, first_token[s] : first_token[s] + s * s].rearrange("p (a b) -> p a b", b=s),
                in0=member[s][:, 0, :].unsqueeze(2).to_broadcast([P, s, s]),
                scalar=float(s * s) / 128.0,
                in1=member[s][:, 1, :].unsqueeze(1).to_broadcast([P, s, s]),
                op0=MULT,
                op1=ADD,
            )
        hits_a = psum.tile([P, LAST, TOKENS], F32, tag="val_23")
        hits_b = psum.tile([P, 1, TOKENS], F32, tag="kf_3")
        for j in range(len(CHUNKS)):
            first = j * P if j < LAST else PAIRS
            nc.tensor.matmul(
                out=hits_a[:, j, :] if j < LAST else hits_b[:, 0, :],
                lhsT=where[:, first : first + P],
                rhs=which[:],
                start=True,
                stop=True,
            )
        nc.vector.memset(pool_mat[:, :, TOKENS:P], 0.0)
        pair = keep.tile([P, PAIRS, HALVES], F32)
        tok = {}
        for s in LEVELS:
            tok[s] = keep.tile([P, s, HALVES, s], F32, name="tok_%d" % s)
        val = keep.tile([P, len(CHUNKS), HALVES * P], F32)

        val_01 = psum.tile([P, 2, HALVES * P], F32, tag="val_01")
        val_acc[0], val_acc[1] = val_01[:, 0, :], val_01[:, 1, :]
        val_23 = psum.tile([P, 2, HALVES * P], F32, tag="val_23")
        val_acc[2], val_acc[3] = val_23[:, 0, :], val_23[:, 1, :]
        kf_acc[0] = psum.tile([P, HALVES, 2 * P], F32, tag="kf_0", name="kf_acc_0")
        kf_acc[1] = psum.tile([P, HALVES, 2 * P], F32, tag="kf_1", name="kf_acc_1")
        kf_acc[2] = psum.tile([P, HALVES, 2 * P], F32, tag="kf_2", name="kf_acc_2")

        regroup(0, 0, nc.vector.tensor_copy)
        regroup(0, 1, nc.scalar.copy)
        nc.vector.tensor_scalar(
            out=pool_mat[:, LAST, 0:TOKENS], in0=hits_b[:, 0, :], scalar1=-1.0, scalar2=0.0, op0=ADD, op1=MAX
        )
        quantise(0)
        idle_bank = psum.tile([P, 4 * P], F32, tag="kf_2", name="idle_bank")
        for half in range(2):
            nc.tensor.matmul(
                out=idle_bank[:],
                lhsT=ident_bf[:],
                rhs=grouped[0][:, 0, half * P : (half + 1) * P, :].rearrange("p c t -> p (c t)"),
                start=True,
                stop=True,
            )
        regroup(1, 1, nc.scalar.copy)
        nc.tensor.matmul(
            out=idle_bank[:],
            lhsT=ident_bf[:],
            rhs=grouped[1][:, 1, 0:P, :].rearrange("p c t -> p (c t)"),
            start=True,
            stop=True,
        )
        vec_t = psum.tile([P, P], BF16, tag="last")
        nc.tensor.transpose(vec_t[:], vec_rows[:], ident_bf[:])
        value_acc = psum.tile([P, HALVES * P], F32, tag="value")
        nc.tensor.matmul(out=value_acc[:], lhsT=nines_bf[:], rhs=bv_row[:], start=True, stop=False)
        project_kf(0)
        regroup(1, 0, nc.vector.tensor_copy)
        regroup(2, 1, nc.scalar.copy)
        inv_std = keep.tile([P, 2], F32)
        nc.scalar.activation(out=inv_std[:], in_=vec_t[:, 8:10], func=ACT.Abs_reciprocal_sqrt, bias=EPS)
        per_ch = keep.tile([P, 8], F32)
        nc.scalar.copy(out=per_ch[:], in_=vec_t[:, 0:8])
        bk_c, gk_c, betak_c, mk_c = [per_ch[:, 2 * v : 2 * v + 2] for v in range(4)]
        nc.scalar.activation(out=pool_mat[:, 0:LAST, 0:TOKENS], in_=hits_a[:], func=ACT.Relu, bias=-1.0)
        quantise(1, slice(1, 2))
        quantise(1, slice(0, 1))
        project_kf(1)
        regroup(2, 0, nc.vector.tensor_copy)
        quantise(2, slice(1, 2))
        centred = keep.tile([P, 2], F32)
        nc.vector.tensor_tensor(out=centred[:], in0=bk_c, in1=mk_c, op=SUBTRACT)
        gain = keep.tile([P, 2], F32)
        nc.vector.tensor_tensor(out=gain[:], in0=inv_std[:], in1=gk_c, op=MULT)
        quantise(2, slice(0, 1))
        shift = keep.tile([P, 2], F32)
        for m in range(HALVES):
            nc.vector.scalar_tensor_tensor(
                out=shift[:, m : m + 1],
                in0=centred[:, m : m + 1],
                scalar=gain[:, m : m + 1],
                in1=betak_c[:, m : m + 1],
                op0=MULT,
                op1=ADD,
            )
        project_kf(2)
        project_val(0)
        project_val(1)
        project_val(2)
        regroup(3, 1, nc.scalar.copy)
        regroup(3, 0, nc.vector.tensor_copy)
        quantise(3, slice(1, 2))
        quantise(3, slice(0, 1))
        kf_acc[3] = psum.tile([P, HALVES, 2 * P], F32, tag="kf_3", name="kf_acc_3")
        project_kf(3)
        norm_relu(0)
        regroup(4, 1, nc.scalar.copy)
        add_pairs(0)
        regroup(4, 0, nc.vector.tensor_copy)
        norm_relu(1)
        pool_row(6, 0)
        quantise(4)
        project_val(3)
        last = psum.tile([P, 4, P], F32, tag="last")
        kf_acc[4], val_acc[4] = last[:, 0:2, :], last[:, 2:4, :].rearrange("p a b -> p (a b)")
        project_kf(4)
        project_val(4)
        keyp = keep.tile([P, HALVES, LEAD + TOKENS], F32)

        def mean(s, a0, a1):
            cells = slice(LEAD + first_token[s] + s * a0, LEAD + first_token[s] + s * a1)
            nc.scalar.mul(
                out=keyp[:, :, cells].rearrange("p q (a b) -> p q a b", b=s),
                in_=tok[s][:, a0:a1, :, :].rearrange("p a q b -> p q a b"),
                mul=float(s * s) / POSITIONS,
            )

        def mean_half(s, a0, a1, q):
            cells = slice(LEAD + first_token[s] + s * a0, LEAD + first_token[s] + s * a1)
            nc.scalar.mul(
                out=keyp[:, q, cells].rearrange("p (a b) -> p a b", b=s),
                in_=tok[s][:, a0:a1, q, :],
                mul=float(s * s) / POSITIONS,
            )

        add_pairs(1)
        pool_row(8, 0)
        pool_rows(8, 1, 3, 0)
        nc.scalar.copy(out=val[:, 0:2, :], in_=val_01[:])
        pool_val(0, False)
        pool_val(1, False)
        pool_row(6, 1)
        norm_relu(2)
        add_pairs(2)
        pool_rows(8, 1, 3, 1)
        pool_level3(0)
        pool_row(6, 2)
        pool_rows(8, 3, 5, 0)
        pool_row(6, 3)
        norm_relu(3)
        add_pairs(3)
        pool_rows(8, 3, 5, 1)
        pool_level3(1)
        nc.scalar.copy(out=val[:, 2:4, :], in_=val_23[:])
        pool_val(2, False)
        pool_val(3, False)
        norm_relu(4)
        pool_rows(8, 5, 7, 0)
        nc.scalar.copy(out=val[:, 4, :], in_=val_acc[4])
        add_pairs(4)
        pool_row(6, 4)
        pool_row(8, 7)
        mean(6, 0, 5)
        pool_row(6, 5)
        pool_rows(8, 5, 7, 1)
        pool_val(4, True)
        before = psum.tile([P, HALVES, LEAD], F32, tag="kf_0")
        nc.tensor.matmul(out=before[:], lhsT=down, rhs=tok[8][:, 7, :, 8 - LEAD : 8], start=True, stop=True)
        for q in range(HALVES):
            mean_half(8, 7, 8, q)
        for q in range(HALVES):
            mean_half(6, 5, 6, q)
        nc.vector.tensor_reduce(
            out=tok[1][:, 0, :, 0], in_=tok[6][:].rearrange("p a q b -> p q a b"), axis=AXIS.XY, op=ADD
        )
        mean(8, 0, 7)
        pool_level3(2)
        for q in range(HALVES):
            nc.scalar.mul(out=keyp[:, q, 0:LEAD], in_=before[:, q, :], mul=64.0 / POSITIONS)
        for q in range(HALVES):
            mean_half(1, 0, 1, q)
        for q in range(HALVES):
            mean_half(3, 0, 3, q)
        value_sb = keep.tile([P, HALVES * P], F32)
        nc.vector.tensor_scalar(out=value_sb[:], in0=value_acc[:], scalar1=1.0 / 9.0, scalar2=None, op0=MULT)
        groups = out_1[0].rearrange("(m q j) t -> q m (j t)", m=HALVES, j=4)
        for j in range(4):
            borrowed, lent = (-2 * j) % 8, (-2 * (j + 1)) % 8
            length = borrowed + TOKENS - lent
            nc.scalar.dma_start(
                out=groups[:, :, TOKENS * j - borrowed : TOKENS * j - borrowed + length],
                in_=keyp[j:P:4, :, LEAD - borrowed : LEAD - borrowed + length],
            )
        for lo, hi in ((96, TOKENS), (0, 64), (64, 96)):
            nc.sync.dma_start(out=out_2[0, lo:hi, :], in_=value_sb[lo:hi, :])
